import numpy as np
import ml_dtypes


def mxq(x, axis, fmt="e4m3"):
    dtype, down = {"e4m3": (ml_dtypes.float8_e4m3fn, 7), "e5m2": (ml_dtypes.float8_e5m2, 14)}[fmt]
    v = np.moveaxis(np.asarray(x, np.float32).astype(ml_dtypes.bfloat16).astype(np.float64), axis, -1)
    blocks = v.reshape(v.shape[:-1] + (-1, 32))
    amax = np.abs(blocks).max(-1, keepdims=True)
    byte = np.maximum(np.where(amax > 0, np.frexp(amax)[1] - 1 + 127, 0) - down, 1)
    scale = np.exp2(byte - 127.0)
    codes = (blocks / scale).astype(np.float32).astype(dtype).astype(np.float64)
    return np.moveaxis((codes * scale).reshape(v.shape), -1, axis)


WIDE = False


def mx_kscale(k, group=512):
    if not WIDE:
        return np.ones(k)
    levels = np.array([20, -20, 10, -10, 0])
    if group != 512:
        return np.exp2(np.random.permutation(np.resize(levels, k // group))).repeat(group)
    a = np.random.permutation(np.resize(levels, k // 512 * 4)).reshape(k // 512, 4)
    idx = np.arange(k)
    return np.exp2(a[idx // 512, idx % 128 // 32])


BF16 = ml_dtypes.bfloat16


def bf(x):
    return np.asarray(x, np.float32).astype(BF16)


def f64(x):
    return np.asarray(x).astype(np.float64)


B, H, W, C, F, K, G, RR = 4, 8, 32, 256, 512, 3, 16, 4
KK = K * K
P = B * H * W


def setup_inputs():
    s = mx_kscale(P, H * W).reshape(B, H * W)[:, 0].reshape(B, 1, 1, 1)
    x = np.random.standard_normal((B, H, W, C)) * s
    Wi = np.random.standard_normal((C, F)) / np.sqrt(C)
    bi = np.random.standard_normal(F) * 0.3
    w_span = np.random.standard_normal((B, H, W, KK * G)) * 0.7
    g = np.random.standard_normal((B, H, W, F)) * np.exp2(np.random.randint(-12, 1, (B, H, W, 1))) * 0.25 / s
    return {"x": bf(x), "Wi": bf(Wi), "bi": bf(bi), "w_span": bf(w_span), "grad_out": bf(g)}


def grad_xi(w_span, grad_out):
    g = f64(grad_out).reshape(B, H, W, G, F // G, 1)
    w = f64(w_span).reshape(B, H, W, G, 1, KK)
    q = (g * w).reshape(B, H, W, KK, F)
    pad = (K - 1) // 2
    gp = np.zeros((B, H + 2 * pad, W + 2 * pad, F))
    for i in range(K):
        for j in range(K):
            gp[:, i:i + H, j:j + W, :] += q[:, :, :, i * K + j, :]
    return gp[:, pad:pad + H, pad:pad + W, :]


def reference(x, Wi, bi, w_span, grad_out):
    gxi = grad_xi(w_span, grad_out).reshape(P, F)
    return mxq(f64(x).reshape(P, C), 0, "e4m3").T @ mxq(gxi, 0, "e5m2")

@@ -1,0 +1,228 @@
+from contextlib import ExitStack
+
+import concourse.mybir as mybir
+from concourse.masks import make_identity
+
+F32 = mybir.dt.float32
+BF16 = mybir.dt.bfloat16
+U32 = mybir.dt.uint32
+U8 = mybir.dt.uint8
+E4M3_X4 = mybir.dt.float8_e4m3fn_x4
+E5M2_X4 = mybir.dt.float8_e5m2_x4
+
+P = 128
+IMAGES, ROWS, COLS = 4, 8, 32
+X_CH = 256
+CH = 512
+GROUPS = 16
+GROUP_CH = CH // GROUPS
+KERNEL = 3
+TAPS = KERNEL * KERNEL
+TILE_ROWS = P // COLS
+IMAGE_TILES = ROWS // TILE_ROWS
+IMAGE_PIXELS = ROWS * COLS
+TILES = IMAGES * IMAGE_TILES
+CH_TILES = CH // P
+BANK_CH_TILES = 2
+SUM_BANKS = CH_TILES // BANK_CH_TILES
+PACK = 4
+PASSES = IMAGES * IMAGE_PIXELS // (P * PACK)
+PASS_IMAGES = IMAGES // PASSES
+IMAGE_WORD_ROWS = IMAGE_PIXELS // PACK
+
+TAP_CH = CH // TAPS + 2
+
+FLOPS = 2 * IMAGES * IMAGE_PIXELS * X_CH * CH + 2 * IMAGES * IMAGE_PIXELS * CH * TAPS
+BYTES = 2 * IMAGES * IMAGE_PIXELS * (X_CH + CH + GROUPS * TAPS) + 4 * X_CH * CH
+
+TAP_ORDER = (4, 0, 1, 2, 3, 5, 6, 7, 8)
+
+
+def tap_channels(t):
+    first = (TAP_CH - 1) * t - 1
+    return first, max(first, 0), min(first + TAP_CH, CH)
+
+
+def tile_involution2d_pa_s_kernel(tc, x, Wi, bi, w_span, grad_out, out):
+    nc = tc.nc
+    with ExitStack() as ctx:
+        keep = ctx.enter_context(tc.tile_pool(name="keep", bufs=1))
+        products = ctx.enter_context(tc.tile_pool(name="products", bufs=4))
+        per_pass = ctx.enter_context(tc.tile_pool(name="per_pass", bufs=2))
+        sums_psum = ctx.enter_context(tc.psum_pool(name="sums_psum", bufs=2))
+        back_psum = ctx.enter_context(tc.psum_pool(name="back_psum", bufs=1))
+        out_psum = ctx.enter_context(tc.psum_pool(name="out_psum", bufs=1))
+
+        g_rows = grad_out.rearrange("b h w f -> (b h w) f").rearrange("(u p) f -> p u f", p=P)
+        w_rows = w_span.rearrange("b h w f -> (b h w) f").rearrange("(u p) f -> p u f", p=P)
+        g_sb = keep.tile([P, TILES, CH], BF16)
+        w_sb = keep.tile([P, TILES, GROUPS * TAPS], BF16)
+        nc.scalar.dma_start(out=w_sb[:], in_=w_rows)
+        for image in range(IMAGES):
+            tiles = slice(image * IMAGE_TILES, (image + 1) * IMAGE_TILES)
+            nc.sync.dma_start(out=g_sb[:, tiles, :], in_=g_rows[:, tiles, :])
+        x_raw = keep.tile([P, PASSES, PACK, X_CH], BF16)
+        nc.scalar.dma_start(
+            out=x_raw[:],
+            in_=x.rearrange("b h w k -> (b h w) k").rearrange("(n p j) k -> p n j k", p=P, j=PACK),
+        )
+
+        ident_twice = keep.tile([P, 2 * P], F32)
+        make_identity(nc, ident_twice[:, 0:P])
+        make_identity(nc, ident_twice[:, P : 2 * P])
+        ident_bf16 = keep.tile([P, P], BF16)
+        make_identity(nc, ident_bf16[:])
+
+        ident_by_col = ident_twice[:, 0:P].rearrange("k (r s) -> k s r", s=COLS)
+        on_edge = keep.tile([P, 2], F32)
+        nc.vector.tensor_reduce(
+            out=on_edge[:, 0:1], in_=ident_by_col[:, 0, :], axis=mybir.AxisListType.X, op=mybir.AluOpType.add
+        )
+        nc.vector.tensor_reduce(
+            out=on_edge[:, 1:2],
+            in_=ident_by_col[:, COLS - 1, :],
+            axis=mybir.AxisListType.X,
+            op=mybir.AluOpType.add,
+        )
+        off_edge = keep.tile([P, 2], F32)
+        nc.vector.tensor_scalar(
+            out=off_edge[:],
+            in0=on_edge[:],
+            scalar1=-1.0,
+            scalar2=1.0,
+            op0=mybir.AluOpType.mult,
+            op1=mybir.AluOpType.add,
+        )
+        has_neighbour = keep.tile([P, IMAGE_TILES, KERNEL, KERNEL], F32)
+        nc.vector.memset(has_neighbour[:], 1.0)
+        for j, edge in ((0, 0), (KERNEL - 1, 1)):
+            nc.vector.tensor_copy(
+                out=has_neighbour[:, :, :, j],
+                in_=off_edge[:, edge : edge + 1].unsqueeze(2).to_broadcast([P, IMAGE_TILES, KERNEL]),
+            )
+        nc.vector.memset(has_neighbour[0:COLS, 0, 0, :], 0.0)
+        nc.vector.memset(has_neighbour[P - COLS : P, IMAGE_TILES - 1, KERNEL - 1, :], 0.0)
+
+        w_tap = keep.tile([P, TILES, TAPS, GROUPS * TAPS], BF16)
+        w_sb_halves = w_sb[:].rearrange("p (b h) f -> p b h f", h=IMAGE_TILES)
+        w_tap_halves = w_tap[:].rearrange("p (b h) t f -> p b h t f", h=IMAGE_TILES)
+        for t in TAP_ORDER:
+            first, ch_lo, ch_hi = tap_channels(t)
+            weights = slice(ch_lo // GROUP_CH * TAPS, ((ch_hi - 1) // GROUP_CH + 1) * TAPS)
+            for half in range(IMAGE_TILES):
+                nc.scalar.activation(
+                    out=w_tap_halves[:, :, half, t, weights],
+                    in_=w_sb_halves[:, :, half, weights],
+                    func=mybir.ActivationFunctionType.Copy,
+                    scale=has_neighbour[:, half, t // KERNEL, t % KERNEL : t % KERNEL + 1],
+                )
+
+        x_grouped = keep.tile([P, PASSES, X_CH, PACK], BF16, align_bytes=64)
+        for n in range(PASSES):
+            nc.scalar.copy(out=x_grouped[:, n], in_=x_raw[:, n].rearrange("p j k -> p k j"))
+        x_codes = keep.tile([P, PASSES, X_CH], U32, align_bytes=64)
+        x_scales = keep.tile([P, PASSES, X_CH], U8, align_bytes=64)
+        nc.vector.quantize_mx(
+            out=x_codes[:].rearrange("p n k -> p (n k)").bitcast(E4M3_X4),
+            scales=x_scales[:].rearrange("p n k -> p (n k)"),
+            in_=x_grouped[:].rearrange("p n k j -> p (n k j)"),
+        )
+
+        out_acc = [out_psum.tile([P, CH], F32, name="out_acc%d" % m) for m in range(X_CH // P)]
+
+        for n in range(PASSES):
+            gxi_t = per_pass.tile([P, CH_TILES, PACK, P], BF16)
+            for image_in_pass in range(PASS_IMAGES):
+                image = n * PASS_IMAGES + image_in_pass
+                tiles = slice(image * IMAGE_TILES, (image + 1) * IMAGE_TILES)
+                sums = [
+                    sums_psum.tile([P, BANK_CH_TILES, IMAGE_PIXELS], F32, name="sums%d" % h)
+                    for h in range(SUM_BANKS)
+                ]
+                for t in TAP_ORDER:
+                    i, j = t // KERNEL, t % KERNEL
+                    first, ch_lo, ch_hi = tap_channels(t)
+                    prod = products.tile([P, IMAGE_TILES, TAP_CH * TAPS], F32)
+                    for group in range(ch_lo // GROUP_CH, (ch_hi - 1) // GROUP_CH + 1):
+                        lo = max(ch_lo, group * GROUP_CH)
+                        hi = min(ch_hi, (group + 1) * GROUP_CH)
+                        shape = [P, IMAGE_TILES, hi - lo, TAPS]
+                        nc.vector.tensor_tensor(
+                            out=prod[:, :, (lo - first) * TAPS : (hi - first) * TAPS].rearrange(
+                                "p h (o m) -> p h o m", m=TAPS
+                            ),
+                            in0=g_sb[:, tiles, lo:hi].unsqueeze(3).to_broadcast(shape),
+                            in1=w_tap[:, tiles, t, group * TAPS : (group + 1) * TAPS]
+                            .unsqueeze(2)
+                            .to_broadcast(shape),
+                            op=mybir.AluOpType.mult,
+                        )
+                    first_col = t * CH - first * TAPS
+                    for half in range(IMAGE_TILES):
+                        wanted = half * P + (i - 1) * COLS
+                        start_pixel = min(max(wanted, 0), IMAGE_PIXELS - P)
+                        turn = (start_pixel - wanted - (j - 1)) % P
+                        for ct in range(CH_TILES):
+                            first_in_bank = ct % BANK_CH_TILES == 0
+                            nc.tensor.matmul(
+                                out=sums[ct // BANK_CH_TILES][
+                                    :, ct % BANK_CH_TILES, start_pixel : start_pixel + P
+                                ],
+                                lhsT=prod[:, half, first_col + ct * P : first_col + (ct + 1) * P],
+                                rhs=ident_twice[:, turn : turn + P],
+                                is_transpose=True,
+                                start=(t == TAP_ORDER[0] and half == 0 and first_in_bank),
+                                stop=(
+                                    t == TAP_ORDER[-1]
+                                    and half == IMAGE_TILES - 1
+                                    and not first_in_bank
+                                ),
+                            )
+                word_rows = slice(
+                    image_in_pass * IMAGE_WORD_ROWS, (image_in_pass + 1) * IMAGE_WORD_ROWS
+                )
+                for h in range(SUM_BANKS):
+                    nc.scalar.copy(
+                        out=gxi_t[:, h * BANK_CH_TILES : (h + 1) * BANK_CH_TILES, :, word_rows],
+                        in_=sums[h][:].rearrange("c t (a j) -> c t j a", j=PACK),
+                    )
+
+            gxi_grouped = per_pass.tile([P, CH, PACK], BF16, align_bytes=64)
+            for h in range(SUM_BANKS):
+                back = back_psum.tile([P, PACK, BANK_CH_TILES * P], BF16, name="back%d" % h)
+                for ct in range(h * BANK_CH_TILES, (h + 1) * BANK_CH_TILES):
+                    for j in range(PACK):
+                        nc.tensor.transpose(
+                            back[:, j, (ct % BANK_CH_TILES) * P : (ct % BANK_CH_TILES + 1) * P],
+                            gxi_t[:, ct, j, :],
+                            ident_bf16[:],
+                        )
+                nc.scalar.copy(
+                    out=gxi_grouped[:, h * BANK_CH_TILES * P : (h + 1) * BANK_CH_TILES * P, :],
+                    in_=back[:].rearrange("p j c -> p c j"),
+                )
+            gxi_codes = per_pass.tile([P, CH], U32, align_bytes=64)
+            gxi_scales = per_pass.tile([P, CH], U8, align_bytes=64)
+            nc.vector.quantize_mx(
+                out=gxi_codes[:].bitcast(E5M2_X4),
+                scales=gxi_scales[:],
+                in_=gxi_grouped[:].rearrange("p c j -> p (c j)"),
+            )
+            for m in range(X_CH // P):
+                nc.tensor.matmul_mx(
+                    out=out_acc[m][:],
+                    lhsT=x_codes[:, n, m * P : (m + 1) * P].bitcast(E4M3_X4),
+                    lhsT_scale=x_scales[:, n, m * P : (m + 1) * P],
+                    rhs=gxi_codes[:].bitcast(E5M2_X4),
+                    rhs_scale=gxi_scales[:],
+                    start=(n == 0),
+                    stop=(n == PASSES - 1),
+                )
+
+        for m in range(X_CH // P):
+            result = keep.tile([P, CH], F32, name="result%d" % m)
+            if m % 2 == 0:
+                nc.scalar.copy(out=result[:], in_=out_acc[m][:])
+            else:
+                nc.vector.tensor_copy(out=result[:], in_=out_acc[m][:])
+            nc.sync.dma_start(out=out[m * P : (m + 1) * P, :], in_=result[:])

@@ -47,7 +47,7 @@ def tile_involution2d_pa_s_kernel(tc, x, Wi, bi, w_span, grad_out, out):
     nc = tc.nc
     with ExitStack() as ctx:
         keep = ctx.enter_context(tc.tile_pool(name="keep", bufs=1))
-        products = ctx.enter_context(tc.tile_pool(name="products", bufs=4))
+        products = ctx.enter_context(tc.tile_pool(name="products", bufs=6))
         per_pass = ctx.enter_context(tc.tile_pool(name="per_pass", bufs=2))
         sums_psum = ctx.enter_context(tc.psum_pool(name="sums_psum", bufs=2))
         back_psum = ctx.enter_context(tc.psum_pool(name="back_psum", bufs=1))
@@ -62,7 +62,7 @@ def tile_involution2d_pa_s_kernel(tc, x, Wi, bi, w_span, grad_out, out):
             tiles = slice(image * IMAGE_TILES, (image + 1) * IMAGE_TILES)
             nc.sync.dma_start(out=g_sb[:, tiles, :], in_=g_rows[:, tiles, :])
         x_raw = keep.tile([P, PASSES, PACK, X_CH], BF16)
-        nc.scalar.dma_start(
+        nc.sync.dma_start(
             out=x_raw[:],
             in_=x.rearrange("b h w k -> (b h w) k").rearrange("(n p j) k -> p n j k", p=P, j=PACK),
         )
@@ -118,15 +118,8 @@ def tile_involution2d_pa_s_kernel(tc, x, Wi, bi, w_span, grad_out, out):
                 )
 
         x_grouped = keep.tile([P, PASSES, X_CH, PACK], BF16, align_bytes=64)
-        for n in range(PASSES):
-            nc.scalar.copy(out=x_grouped[:, n], in_=x_raw[:, n].rearrange("p j k -> p k j"))
         x_codes = keep.tile([P, PASSES, X_CH], U32, align_bytes=64)
         x_scales = keep.tile([P, PASSES, X_CH], U8, align_bytes=64)
-        nc.vector.quantize_mx(
-            out=x_codes[:].rearrange("p n k -> p (n k)").bitcast(E4M3_X4),
-            scales=x_scales[:].rearrange("p n k -> p (n k)"),
-            in_=x_grouped[:].rearrange("p n k j -> p (n k j)"),
-        )
 
         out_acc = [out_psum.tile([P, CH], F32, name="out_acc%d" % m) for m in range(X_CH // P)]
 
@@ -158,12 +151,12 @@ def tile_involution2d_pa_s_kernel(tc, x, Wi, bi, w_span, grad_out, out):
                             op=mybir.AluOpType.mult,
                         )
                     first_col = t * CH - first * TAPS
-                    for half in range(IMAGE_TILES):
-                        wanted = half * P + (i - 1) * COLS
-                        start_pixel = min(max(wanted, 0), IMAGE_PIXELS - P)
-                        turn = (start_pixel - wanted - (j - 1)) % P
-                        for ct in range(CH_TILES):
-                            first_in_bank = ct % BANK_CH_TILES == 0
+                    for ct in range(CH_TILES):
+                        first_in_bank = ct % BANK_CH_TILES == 0
+                        for half in range(IMAGE_TILES):
+                            wanted = half * P + (i - 1) * COLS
+                            start_pixel = min(max(wanted, 0), IMAGE_PIXELS - P)
+                            turn = (start_pixel - wanted - (j - 1)) % P
                             nc.tensor.matmul(
                                 out=sums[ct // BANK_CH_TILES][
                                     :, ct % BANK_CH_TILES, start_pixel : start_pixel + P
@@ -182,10 +175,22 @@ def tile_involution2d_pa_s_kernel(tc, x, Wi, bi, w_span, grad_out, out):
                     image_in_pass * IMAGE_WORD_ROWS, (image_in_pass + 1) * IMAGE_WORD_ROWS
                 )
                 for h in range(SUM_BANKS):
-                    nc.scalar.copy(
+                    copy_out = nc.vector.tensor_copy if image == IMAGES - 1 and h == 1 else nc.scalar.copy
+                    copy_out(
                         out=gxi_t[:, h * BANK_CH_TILES : (h + 1) * BANK_CH_TILES, :, word_rows],
                         in_=sums[h][:].rearrange("c t (a j) -> c t j a", j=PACK),
                     )
+
+            if n == 0:
+                for x_pass in range(PASSES):
+                    nc.scalar.copy(
+                        out=x_grouped[:, x_pass], in_=x_raw[:, x_pass].rearrange("p j k -> p k j")
+                    )
+                nc.vector.quantize_mx(
+                    out=x_codes[:].rearrange("p n k -> p (n k)").bitcast(E4M3_X4),
+                    scales=x_scales[:].rearrange("p n k -> p (n k)"),
+                    in_=x_grouped[:].rearrange("p n k j -> p (n k j)"),
+                )
 
             gxi_grouped = per_pass.tile([P, CH, PACK], BF16, align_bytes=64)
             for h in range(SUM_BANKS):
@@ -197,7 +202,8 @@ def tile_involution2d_pa_s_kernel(tc, x, Wi, bi, w_span, grad_out, out):
                             gxi_t[:, ct, j, :],
                             ident_bf16[:],
                         )
-                nc.scalar.copy(
+                copy_out = nc.vector.tensor_copy if n == PASSES - 1 and h == 1 else nc.scalar.copy
+                copy_out(
                     out=gxi_grouped[:, h * BANK_CH_TILES * P : (h + 1) * BANK_CH_TILES * P, :],
                     in_=back[:].rearrange("p j c -> p c j"),
                 )

@@ -36,6 +36,8 @@ FLOPS = 2 * IMAGES * IMAGE_PIXELS * X_CH * CH + 2 * IMAGES * IMAGE_PIXELS * CH *
 BYTES = 2 * IMAGES * IMAGE_PIXELS * (X_CH + CH + GROUPS * TAPS) + 4 * X_CH * CH
 
 TAP_ORDER = (4, 0, 1, 2, 3, 5, 6, 7, 8)
+FINISH_STAGES = 3
+FINISH_LAG = 2
 
 
 def tap_channels(t):
@@ -57,7 +59,7 @@ def tile_involution2d_pa_s_kernel(tc, x, Wi, bi, w_span, grad_out, out):
         w_rows = w_span.rearrange("b h w f -> (b h w) f").rearrange("(u p) f -> p u f", p=P)
         g_sb = keep.tile([P, TILES, CH], BF16)
         w_sb = keep.tile([P, TILES, GROUPS * TAPS], BF16)
-        nc.scalar.dma_start(out=w_sb[:], in_=w_rows)
+        nc.sync.dma_start(out=w_sb[:], in_=w_rows)
         for image in range(IMAGES):
             tiles = slice(image * IMAGE_TILES, (image + 1) * IMAGE_TILES)
             nc.sync.dma_start(out=g_sb[:, tiles, :], in_=g_rows[:, tiles, :])
@@ -106,7 +108,7 @@ def tile_involution2d_pa_s_kernel(tc, x, Wi, bi, w_span, grad_out, out):
         w_tap = keep.tile([P, TILES, TAPS, GROUPS * TAPS], BF16)
         w_sb_halves = w_sb[:].rearrange("p (b h) f -> p b h f", h=IMAGE_TILES)
         w_tap_halves = w_tap[:].rearrange("p (b h) t f -> p b h t f", h=IMAGE_TILES)
-        for t in TAP_ORDER:
+        for t in TAP_ORDER[1:]:
             first, ch_lo, ch_hi = tap_channels(t)
             weights = slice(ch_lo // GROUP_CH * TAPS, ((ch_hi - 1) // GROUP_CH + 1) * TAPS)
             for half in range(IMAGE_TILES):
@@ -121,99 +123,87 @@ def tile_involution2d_pa_s_kernel(tc, x, Wi, bi, w_span, grad_out, out):
         x_codes = keep.tile([P, PASSES, X_CH], U32, align_bytes=64)
         x_scales = keep.tile([P, PASSES, X_CH], U8, align_bytes=64)
 
-        out_acc = [out_psum.tile([P, CH], F32, name="out_acc%d" % m) for m in range(X_CH // P)]
+        def quantise_x():
+            for n in range(PASSES):
+                nc.scalar.copy(out=x_grouped[:, n], in_=x_raw[:, n].rearrange("p j k -> p k j"))
+            nc.vector.quantize_mx(
+                out=x_codes[:].rearrange("p n k -> p (n k)").bitcast(E4M3_X4),
+                scales=x_scales[:].rearrange("p n k -> p (n k)"),
+                in_=x_grouped[:].rearrange("p n k j -> p (n k j)"),
+            )
 
-        for n in range(PASSES):
-            gxi_t = per_pass.tile([P, CH_TILES, PACK, P], BF16)
-            for image_in_pass in range(PASS_IMAGES):
-                image = n * PASS_IMAGES + image_in_pass
-                tiles = slice(image * IMAGE_TILES, (image + 1) * IMAGE_TILES)
-                sums = [
-                    sums_psum.tile([P, BANK_CH_TILES, IMAGE_PIXELS], F32, name="sums%d" % h)
-                    for h in range(SUM_BANKS)
-                ]
-                for t in TAP_ORDER:
-                    i, j = t // KERNEL, t % KERNEL
-                    first, ch_lo, ch_hi = tap_channels(t)
-                    prod = products.tile([P, IMAGE_TILES, TAP_CH * TAPS], F32)
-                    for group in range(ch_lo // GROUP_CH, (ch_hi - 1) // GROUP_CH + 1):
-                        lo = max(ch_lo, group * GROUP_CH)
-                        hi = min(ch_hi, (group + 1) * GROUP_CH)
-                        shape = [P, IMAGE_TILES, hi - lo, TAPS]
-                        nc.vector.tensor_tensor(
-                            out=prod[:, :, (lo - first) * TAPS : (hi - first) * TAPS].rearrange(
-                                "p h (o m) -> p h o m", m=TAPS
-                            ),
-                            in0=g_sb[:, tiles, lo:hi].unsqueeze(3).to_broadcast(shape),
-                            in1=w_tap[:, tiles, t, group * TAPS : (group + 1) * TAPS]
-                            .unsqueeze(2)
-                            .to_broadcast(shape),
-                            op=mybir.AluOpType.mult,
-                        )
-                    first_col = t * CH - first * TAPS
-                    for ct in range(CH_TILES):
-                        first_in_bank = ct % BANK_CH_TILES == 0
-                        for half in range(IMAGE_TILES):
-                            wanted = half * P + (i - 1) * COLS
-                            start_pixel = min(max(wanted, 0), IMAGE_PIXELS - P)
-                            turn = (start_pixel - wanted - (j - 1)) % P
-                            nc.tensor.matmul(
-                                out=sums[ct // BANK_CH_TILES][
-                                    :, ct % BANK_CH_TILES, start_pixel : start_pixel + P
-                                ],
-                                lhsT=prod[:, half, first_col + ct * P : first_col + (ct + 1) * P],
-                                rhs=ident_twice[:, turn : turn + P],
-                                is_transpose=True,
-                                start=(t == TAP_ORDER[0] and half == 0 and first_in_bank),
-                                stop=(
-                                    t == TAP_ORDER[-1]
-                                    and half == IMAGE_TILES - 1
-                                    and not first_in_bank
-                                ),
-                            )
-                word_rows = slice(
-                    image_in_pass * IMAGE_WORD_ROWS, (image_in_pass + 1) * IMAGE_WORD_ROWS
+        def multiply_tap(image, t):
+            tiles = slice(image * IMAGE_TILES, (image + 1) * IMAGE_TILES)
+            first, ch_lo, ch_hi = tap_channels(t)
+            prod = products.tile([P, IMAGE_TILES, TAP_CH * TAPS], F32)
+            weights = w_sb[:, tiles, :] if t == TAP_ORDER[0] else w_tap[:, tiles, t, :]
+            for group in range(ch_lo // GROUP_CH, (ch_hi - 1) // GROUP_CH + 1):
+                lo = max(ch_lo, group * GROUP_CH)
+                hi = min(ch_hi, (group + 1) * GROUP_CH)
+                shape = [P, IMAGE_TILES, hi - lo, TAPS]
+                nc.vector.tensor_tensor(
+                    out=prod[:, :, (lo - first) * TAPS : (hi - first) * TAPS].rearrange(
+                        "p h (o m) -> p h o m", m=TAPS
+                    ),
+                    in0=g_sb[:, tiles, lo:hi].unsqueeze(3).to_broadcast(shape),
+                    in1=weights[:, :, group * TAPS : (group + 1) * TAPS]
+                    .unsqueeze(2)
+                    .to_broadcast(shape),
+                    op=mybir.AluOpType.mult,
                 )
-                for h in range(SUM_BANKS):
-                    copy_out = nc.vector.tensor_copy if image == IMAGES - 1 and h == 1 else nc.scalar.copy
-                    copy_out(
-                        out=gxi_t[:, h * BANK_CH_TILES : (h + 1) * BANK_CH_TILES, :, word_rows],
-                        in_=sums[h][:].rearrange("c t (a j) -> c t j a", j=PACK),
+            return prod
+
+        def add_tap(sums, prod, t):
+            i, j = t // KERNEL, t % KERNEL
+            first_col = t * CH - tap_channels(t)[0] * TAPS
+            for ct in range(CH_TILES):
+                first_in_bank = ct % BANK_CH_TILES == 0
+                for half in range(IMAGE_TILES):
+                    wanted = half * P + (i - 1) * COLS
+                    start_pixel = min(max(wanted, 0), IMAGE_PIXELS - P)
+                    turn = (start_pixel - wanted - (j - 1)) % P
+                    nc.tensor.matmul(
+                        out=sums[ct // BANK_CH_TILES][
+                            :, ct % BANK_CH_TILES, start_pixel : start_pixel + P
+                        ],
+                        lhsT=prod[:, half, first_col + ct * P : first_col + (ct + 1) * P],
+                        rhs=ident_twice[:, turn : turn + P],
+                        is_transpose=True,
+                        start=(t == TAP_ORDER[0] and half == 0 and first_in_bank),
+                        stop=(t == TAP_ORDER[-1] and half == IMAGE_TILES - 1 and not first_in_bank),
                     )
 
-            if n == 0:
-                for x_pass in range(PASSES):
-                    nc.scalar.copy(
-                        out=x_grouped[:, x_pass], in_=x_raw[:, x_pass].rearrange("p j k -> p k j")
-                    )
-                nc.vector.quantize_mx(
-                    out=x_codes[:].rearrange("p n k -> p (n k)").bitcast(E4M3_X4),
-                    scales=x_scales[:].rearrange("p n k -> p (n k)"),
-                    in_=x_grouped[:].rearrange("p n k j -> p (n k j)"),
-                )
+        def second_copy(last):
+            return nc.vector.tensor_copy if last else nc.scalar.copy
 
-            gxi_grouped = per_pass.tile([P, CH, PACK], BF16, align_bytes=64)
+        def back_to_pixels(n, gxi_t, gxi_grouped):
             for h in range(SUM_BANKS):
                 back = back_psum.tile([P, PACK, BANK_CH_TILES * P], BF16, name="back%d" % h)
-                for ct in range(h * BANK_CH_TILES, (h + 1) * BANK_CH_TILES):
+                for ct in range(BANK_CH_TILES):
                     for j in range(PACK):
                         nc.tensor.transpose(
-                            back[:, j, (ct % BANK_CH_TILES) * P : (ct % BANK_CH_TILES + 1) * P],
-                            gxi_t[:, ct, j, :],
+                            back[:, j, ct * P : (ct + 1) * P],
+                            gxi_t[:, h * BANK_CH_TILES + ct, j, :],
                             ident_bf16[:],
                         )
-                copy_out = nc.vector.tensor_copy if n == PASSES - 1 and h == 1 else nc.scalar.copy
+                copy_out = nc.scalar.copy if h == 0 else second_copy(n == PASSES - 1)
                 copy_out(
                     out=gxi_grouped[:, h * BANK_CH_TILES * P : (h + 1) * BANK_CH_TILES * P, :],
                     in_=back[:].rearrange("p j c -> p c j"),
                 )
-            gxi_codes = per_pass.tile([P, CH], U32, align_bytes=64)
-            gxi_scales = per_pass.tile([P, CH], U8, align_bytes=64)
-            nc.vector.quantize_mx(
-                out=gxi_codes[:].bitcast(E5M2_X4),
-                scales=gxi_scales[:],
-                in_=gxi_grouped[:].rearrange("p c j -> p (c j)"),
-            )
+
+        def quantise_gxi(gxi_grouped, gxi_codes, gxi_scales):
+            for h in range(SUM_BANKS):
+                bank_ch = slice(h * BANK_CH_TILES * P, (h + 1) * BANK_CH_TILES * P)
+                nc.vector.quantize_mx(
+                    out=gxi_codes[:, bank_ch].bitcast(E5M2_X4),
+                    scales=gxi_scales[:, bank_ch],
+                    in_=gxi_grouped[:, bank_ch, :].rearrange("p c j -> p (c j)"),
+                )
+
+        out_acc = [out_psum.tile([P, CH], F32, name="out_acc%d" % m) for m in range(X_CH // P)]
+
+        def multiply_pass(n, gxi_codes, gxi_scales):
             for m in range(X_CH // P):
                 nc.tensor.matmul_mx(
                     out=out_acc[m][:],
@@ -225,10 +215,57 @@ def tile_involution2d_pa_s_kernel(tc, x, Wi, bi, w_span, grad_out, out):
                     stop=(n == PASSES - 1),
                 )
 
+        def finish_stage(stage, n, tiles_of_pass):
+            gxi_t, gxi_grouped, gxi_codes, gxi_scales = tiles_of_pass
+            if stage == 0:
+                back_to_pixels(n, gxi_t, gxi_grouped)
+            elif stage == 1:
+                quantise_gxi(gxi_grouped, gxi_codes, gxi_scales)
+            else:
+                multiply_pass(n, gxi_codes, gxi_scales)
+
+        tiles_of_pass = None
+        for n in range(PASSES):
+            earlier_pass = tiles_of_pass
+            tiles_of_pass = (
+                per_pass.tile([P, CH_TILES, PACK, P], BF16, name="gxi_t"),
+                per_pass.tile([P, CH, PACK], BF16, name="gxi_grouped", align_bytes=64),
+                per_pass.tile([P, CH], U32, name="gxi_codes", align_bytes=64),
+                per_pass.tile([P, CH], U8, name="gxi_scales", align_bytes=64),
+            )
+            for image_in_pass in range(PASS_IMAGES):
+                image = n * PASS_IMAGES + image_in_pass
+                sums = [
+                    sums_psum.tile([P, BANK_CH_TILES, IMAGE_PIXELS], F32, name="sums%d" % h)
+                    for h in range(SUM_BANKS)
+                ]
+                for step, t in enumerate(TAP_ORDER):
+                    add_tap(sums, multiply_tap(image, t), t)
+                    if earlier_pass is not None and image_in_pass == 0 and (step + 1) % FINISH_LAG == 0:
+                        stage = (step + 1) // FINISH_LAG - 1
+                        if stage < FINISH_STAGES:
+                            finish_stage(stage, n - 1, earlier_pass)
+                word_rows = slice(
+                    image_in_pass * IMAGE_WORD_ROWS, (image_in_pass + 1) * IMAGE_WORD_ROWS
+                )
+                for h in range(SUM_BANKS):
+                    copy_out = nc.scalar.copy if h == 0 else second_copy(image == IMAGES - 1)
+                    copy_out(
+                        out=tiles_of_pass[0][
+                            :, h * BANK_CH_TILES : (h + 1) * BANK_CH_TILES, :, word_rows
+                        ],
+                        in_=sums[h][:].rearrange("c t (a j) -> c t j a", j=PACK),
+                    )
+                if image == 0:
+                    quantise_x()
+        for stage in range(FINISH_STAGES):
+            finish_stage(stage, PASSES - 1, tiles_of_pass)
+
         for m in range(X_CH // P):
             result = keep.tile([P, CH], F32, name="result%d" % m)
             if m % 2 == 0:
                 nc.scalar.copy(out=result[:], in_=out_acc[m][:])
+                nc.scalar.dma_start(out=out[m * P : (m + 1) * P, :], in_=result[:])
             else:
                 nc.vector.tensor_copy(out=result[:], in_=out_acc[m][:])
-            nc.sync.dma_start(out=out[m * P : (m + 1) * P, :], in_=result[:])
+                nc.sync.dma_start(out=out[m * P : (m + 1) * P, :], in_=result[:])

@@ -28,6 +28,7 @@ SUM_BANKS = CH_TILES // BANK_CH_TILES
 PACK = 4
 PASSES = IMAGES * IMAGE_PIXELS // (P * PACK)
 PASS_IMAGES = IMAGES // PASSES
+PASS_TILES = PASS_IMAGES * IMAGE_TILES
 IMAGE_WORD_ROWS = IMAGE_PIXELS // PACK
 
 TAP_CH = CH // TAPS + 2
@@ -37,7 +38,6 @@ BYTES = 2 * IMAGES * IMAGE_PIXELS * (X_CH + CH + GROUPS * TAPS) + 4 * X_CH * CH
 
 TAP_ORDER = (4, 0, 1, 2, 3, 5, 6, 7, 8)
 FINISH_STAGES = 3
-FINISH_LAG = 2
 
 
 def tap_channels(t):
@@ -49,7 +49,7 @@ def tile_involution2d_pa_s_kernel(tc, x, Wi, bi, w_span, grad_out, out):
     nc = tc.nc
     with ExitStack() as ctx:
         keep = ctx.enter_context(tc.tile_pool(name="keep", bufs=1))
-        products = ctx.enter_context(tc.tile_pool(name="products", bufs=6))
+        products = ctx.enter_context(tc.tile_pool(name="products", bufs=4))
         per_pass = ctx.enter_context(tc.tile_pool(name="per_pass", bufs=2))
         sums_psum = ctx.enter_context(tc.psum_pool(name="sums_psum", bufs=2))
         back_psum = ctx.enter_context(tc.psum_pool(name="back_psum", bufs=1))
@@ -132,15 +132,15 @@ def tile_involution2d_pa_s_kernel(tc, x, Wi, bi, w_span, grad_out, out):
                 in_=x_grouped[:].rearrange("p n k j -> p (n k j)"),
             )
 
-        def multiply_tap(image, t):
-            tiles = slice(image * IMAGE_TILES, (image + 1) * IMAGE_TILES)
+        def multiply_tap(n, t):
+            tiles = slice(n * PASS_TILES, (n + 1) * PASS_TILES)
             first, ch_lo, ch_hi = tap_channels(t)
-            prod = products.tile([P, IMAGE_TILES, TAP_CH * TAPS], F32)
+            prod = products.tile([P, PASS_TILES, TAP_CH * TAPS], F32)
             weights = w_sb[:, tiles, :] if t == TAP_ORDER[0] else w_tap[:, tiles, t, :]
             for group in range(ch_lo // GROUP_CH, (ch_hi - 1) // GROUP_CH + 1):
                 lo = max(ch_lo, group * GROUP_CH)
                 hi = min(ch_hi, (group + 1) * GROUP_CH)
-                shape = [P, IMAGE_TILES, hi - lo, TAPS]
+                shape = [P, PASS_TILES, hi - lo, TAPS]
                 nc.vector.tensor_tensor(
                     out=prod[:, :, (lo - first) * TAPS : (hi - first) * TAPS].rearrange(
                         "p h (o m) -> p h o m", m=TAPS
@@ -153,20 +153,22 @@ def tile_involution2d_pa_s_kernel(tc, x, Wi, bi, w_span, grad_out, out):
                 )
             return prod
 
-        def add_tap(sums, prod, t):
+        def add_tap(bank, h, prod, image_in_pass, t):
             i, j = t // KERNEL, t % KERNEL
             first_col = t * CH - tap_channels(t)[0] * TAPS
-            for ct in range(CH_TILES):
+            for ct in range(h * BANK_CH_TILES, (h + 1) * BANK_CH_TILES):
                 first_in_bank = ct % BANK_CH_TILES == 0
                 for half in range(IMAGE_TILES):
                     wanted = half * P + (i - 1) * COLS
                     start_pixel = min(max(wanted, 0), IMAGE_PIXELS - P)
                     turn = (start_pixel - wanted - (j - 1)) % P
                     nc.tensor.matmul(
-                        out=sums[ct // BANK_CH_TILES][
-                            :, ct % BANK_CH_TILES, start_pixel : start_pixel + P
+                        out=bank[:, ct % BANK_CH_TILES, start_pixel : start_pixel + P],
+                        lhsT=prod[
+                            :,
+                            image_in_pass * IMAGE_TILES + half,
+                            first_col + ct * P : first_col + (ct + 1) * P,
                         ],
-                        lhsT=prod[:, half, first_col + ct * P : first_col + (ct + 1) * P],
                         rhs=ident_twice[:, turn : turn + P],
                         is_transpose=True,
                         start=(t == TAP_ORDER[0] and half == 0 and first_in_bank),
@@ -233,31 +235,34 @@ def tile_involution2d_pa_s_kernel(tc, x, Wi, bi, w_span, grad_out, out):
                 per_pass.tile([P, CH], U32, name="gxi_codes", align_bytes=64),
                 per_pass.tile([P, CH], U8, name="gxi_scales", align_bytes=64),
             )
-            for image_in_pass in range(PASS_IMAGES):
-                image = n * PASS_IMAGES + image_in_pass
-                sums = [
+            sums = [
+                [
                     sums_psum.tile([P, BANK_CH_TILES, IMAGE_PIXELS], F32, name="sums%d" % h)
                     for h in range(SUM_BANKS)
                 ]
-                for step, t in enumerate(TAP_ORDER):
-                    add_tap(sums, multiply_tap(image, t), t)
-                    if earlier_pass is not None and image_in_pass == 0 and (step + 1) % FINISH_LAG == 0:
-                        stage = (step + 1) // FINISH_LAG - 1
-                        if stage < FINISH_STAGES:
-                            finish_stage(stage, n - 1, earlier_pass)
-                word_rows = slice(
-                    image_in_pass * IMAGE_WORD_ROWS, (image_in_pass + 1) * IMAGE_WORD_ROWS
-                )
+                for image_in_pass in range(PASS_IMAGES)
+            ]
+            for step, t in enumerate(TAP_ORDER):
+                prod = multiply_tap(n, t)
                 for h in range(SUM_BANKS):
-                    copy_out = nc.scalar.copy if h == 0 else second_copy(image == IMAGES - 1)
+                    for image_in_pass in range(PASS_IMAGES):
+                        add_tap(sums[image_in_pass][h], h, prod, image_in_pass, t)
+                if earlier_pass is not None and step < FINISH_STAGES:
+                    finish_stage(step, n - 1, earlier_pass)
+            for h in range(SUM_BANKS):
+                for image_in_pass in range(PASS_IMAGES):
+                    word_rows = slice(
+                        image_in_pass * IMAGE_WORD_ROWS, (image_in_pass + 1) * IMAGE_WORD_ROWS
+                    )
+                    copy_out = nc.scalar.copy if image_in_pass == 0 else second_copy(n == PASSES - 1)
                     copy_out(
                         out=tiles_of_pass[0][
                             :, h * BANK_CH_TILES : (h + 1) * BANK_CH_TILES, :, word_rows
                         ],
-                        in_=sums[h][:].rearrange("c t (a j) -> c t j a", j=PACK),
+                        in_=sums[image_in_pass][h][:].rearrange("c t (a j) -> c t j a", j=PACK),
                     )
-                if image == 0:
-                    quantise_x()
+            if n == 0:
+                quantise_x()
         for stage in range(FINISH_STAGES):
             finish_stage(stage, PASSES - 1, tiles_of_pass)
 

@@ -22,9 +22,9 @@ TILE_ROWS = P // COLS
 IMAGE_TILES = ROWS // TILE_ROWS
 IMAGE_PIXELS = ROWS * COLS
 TILES = IMAGES * IMAGE_TILES
-CH_TILES = CH // P
 BANK_CH_TILES = 2
-SUM_BANKS = CH_TILES // BANK_CH_TILES
+HALF_CH = BANK_CH_TILES * P
+HALVES = CH // HALF_CH
 PACK = 4
 PASSES = IMAGES * IMAGE_PIXELS // (P * PACK)
 PASS_IMAGES = IMAGES // PASSES
@@ -32,12 +32,15 @@ PASS_TILES = PASS_IMAGES * IMAGE_TILES
 IMAGE_WORD_ROWS = IMAGE_PIXELS // PACK
 
 TAP_CH = CH // TAPS + 2
+HALF_TAP_CH = HALF_CH // TAPS + 2
 
 FLOPS = 2 * IMAGES * IMAGE_PIXELS * X_CH * CH + 2 * IMAGES * IMAGE_PIXELS * CH * TAPS
 BYTES = 2 * IMAGES * IMAGE_PIXELS * (X_CH + CH + GROUPS * TAPS) + 4 * X_CH * CH
 
-TAP_ORDER = (4, 0, 1, 2, 3, 5, 6, 7, 8)
-FINISH_STAGES = 3
+MIDDLE = 4
+POOL_TAPS = (0, 1, 2)
+TAP_ORDER = (4, 3, 0, 5, 6, 1, 7, 8, 2)
+W_IN_PSUM = len(POOL_TAPS) > 0
 
 
 def tap_channels(t):
@@ -45,14 +48,26 @@ def tap_channels(t):
     return first, max(first, 0), min(first + TAP_CH, CH)
 
 
+def tap_groups(t):
+    first, ch_lo, ch_hi = tap_channels(t)
+    return ch_lo // GROUP_CH, (ch_hi - 1) // GROUP_CH + 1
+
+
+PSUM_GROUP_LO = min(tap_groups(t)[0] for t in range(TAPS) if t not in POOL_TAPS)
+PSUM_GROUP_HI = max(tap_groups(t)[1] for t in range(TAPS) if t not in POOL_TAPS)
+PSUM_W = (PSUM_GROUP_HI - PSUM_GROUP_LO) * TAPS
+
+
 def tile_involution2d_pa_s_kernel(tc, x, Wi, bi, w_span, grad_out, out):
     nc = tc.nc
     with ExitStack() as ctx:
         keep = ctx.enter_context(tc.tile_pool(name="keep", bufs=1))
-        products = ctx.enter_context(tc.tile_pool(name="products", bufs=4))
+        dve_products = ctx.enter_context(tc.tile_pool(name="dve_products", bufs=4))
+        pool_products = ctx.enter_context(tc.tile_pool(name="pool_products", bufs=3))
         per_pass = ctx.enter_context(tc.tile_pool(name="per_pass", bufs=2))
-        sums_psum = ctx.enter_context(tc.psum_pool(name="sums_psum", bufs=2))
+        sums_psum = ctx.enter_context(tc.psum_pool(name="sums_psum", bufs=4))
         back_psum = ctx.enter_context(tc.psum_pool(name="back_psum", bufs=1))
+        w_psum = ctx.enter_context(tc.psum_pool(name="w_psum", bufs=1))
         out_psum = ctx.enter_context(tc.psum_pool(name="out_psum", bufs=1))
 
         g_rows = grad_out.rearrange("b h w f -> (b h w) f").rearrange("(u p) f -> p u f", p=P)
@@ -69,11 +84,28 @@ def tile_involution2d_pa_s_kernel(tc, x, Wi, bi, w_span, grad_out, out):
             in_=x.rearrange("b h w k -> (b h w) k").rearrange("(n p j) k -> p n j k", p=P, j=PACK),
         )
 
+        warm = keep.tile([P, 2], F32)
+        nc.vector.memset(warm[:], 0.0)
+        nc.scalar.activation(out=warm[:, 1:2], in_=warm[:, 0:1], func=mybir.ActivationFunctionType.Copy)
+
+        ident_bf16 = keep.tile([P, P], BF16)
+        make_identity(nc, ident_bf16[:])
         ident_twice = keep.tile([P, 2 * P], F32)
         make_identity(nc, ident_twice[:, 0:P])
         make_identity(nc, ident_twice[:, P : 2 * P])
-        ident_bf16 = keep.tile([P, P], BF16)
-        make_identity(nc, ident_bf16[:])
+
+        w_ps = None
+        if W_IN_PSUM:
+            w_ps = w_psum.tile([P, TILES, PSUM_W], BF16, name="w_bank")
+            for n in range(PASSES):
+                tiles = slice(n * PASS_TILES, (n + 1) * PASS_TILES)
+                nc.tensor.matmul(
+                    out=w_ps[:, tiles, :],
+                    lhsT=ident_bf16[:],
+                    rhs=w_sb[:, tiles, PSUM_GROUP_LO * TAPS : PSUM_GROUP_HI * TAPS],
+                    start=True,
+                    stop=True,
+                )
 
         ident_by_col = ident_twice[:, 0:P].rearrange("k (r s) -> k s r", s=COLS)
         on_edge = keep.tile([P, 2], F32)
@@ -105,65 +137,81 @@ def tile_involution2d_pa_s_kernel(tc, x, Wi, bi, w_span, grad_out, out):
         nc.vector.memset(has_neighbour[0:COLS, 0, 0, :], 0.0)
         nc.vector.memset(has_neighbour[P - COLS : P, IMAGE_TILES - 1, KERNEL - 1, :], 0.0)
 
-        w_tap = keep.tile([P, TILES, TAPS, GROUPS * TAPS], BF16)
-        w_sb_halves = w_sb[:].rearrange("p (b h) f -> p b h f", h=IMAGE_TILES)
-        w_tap_halves = w_tap[:].rearrange("p (b h) t f -> p b h t f", h=IMAGE_TILES)
-        for t in TAP_ORDER[1:]:
-            first, ch_lo, ch_hi = tap_channels(t)
-            weights = slice(ch_lo // GROUP_CH * TAPS, ((ch_hi - 1) // GROUP_CH + 1) * TAPS)
-            for half in range(IMAGE_TILES):
-                nc.scalar.activation(
-                    out=w_tap_halves[:, :, half, t, weights],
-                    in_=w_sb_halves[:, :, half, weights],
-                    func=mybir.ActivationFunctionType.Copy,
-                    scale=has_neighbour[:, half, t // KERNEL, t % KERNEL : t % KERNEL + 1],
-                )
+        g_tap = keep.tile([P, TILES, TAPS, TAP_CH], BF16)
+        g_sb_halves = g_sb[:].rearrange("p (b h) f -> p b h f", h=IMAGE_TILES)
+        g_tap_halves = g_tap[:].rearrange("p (b h) t f -> p b h t f", h=IMAGE_TILES)
+        for n in range(PASSES):
+            images = slice(n * PASS_IMAGES, (n + 1) * PASS_IMAGES)
+            for t in TAP_ORDER:
+                if t == MIDDLE:
+                    continue
+                first, ch_lo, ch_hi = tap_channels(t)
+                for half in range(IMAGE_TILES):
+                    nc.scalar.activation(
+                        out=g_tap_halves[:, images, half, t, ch_lo - first : ch_hi - first],
+                        in_=g_sb_halves[:, images, half, ch_lo:ch_hi],
+                        func=mybir.ActivationFunctionType.Copy,
+                        scale=has_neighbour[:, half, t // KERNEL, t % KERNEL : t % KERNEL + 1],
+                    )
 
         x_grouped = keep.tile([P, PASSES, X_CH, PACK], BF16, align_bytes=64)
         x_codes = keep.tile([P, PASSES, X_CH], U32, align_bytes=64)
         x_scales = keep.tile([P, PASSES, X_CH], U8, align_bytes=64)
 
-        def quantise_x():
+        def group_x():
             for n in range(PASSES):
                 nc.scalar.copy(out=x_grouped[:, n], in_=x_raw[:, n].rearrange("p j k -> p k j"))
+
+        def quantise_x():
             nc.vector.quantize_mx(
                 out=x_codes[:].rearrange("p n k -> p (n k)").bitcast(E4M3_X4),
                 scales=x_scales[:].rearrange("p n k -> p (n k)"),
                 in_=x_grouped[:].rearrange("p n k j -> p (n k j)"),
             )
 
-        def multiply_tap(n, t):
+        def multiply_tap(n, h, t):
             tiles = slice(n * PASS_TILES, (n + 1) * PASS_TILES)
-            first, ch_lo, ch_hi = tap_channels(t)
-            prod = products.tile([P, PASS_TILES, TAP_CH * TAPS], F32)
-            weights = w_sb[:, tiles, :] if t == TAP_ORDER[0] else w_tap[:, tiles, t, :]
-            for group in range(ch_lo // GROUP_CH, (ch_hi - 1) // GROUP_CH + 1):
-                lo = max(ch_lo, group * GROUP_CH)
-                hi = min(ch_hi, (group + 1) * GROUP_CH)
+            first_product = t * CH + h * HALF_CH
+            o_lo = first_product // TAPS
+            o_hi = (first_product + HALF_CH - 1) // TAPS + 1
+            on_pool = t in POOL_TAPS
+            if on_pool:
+                prod = pool_products.tile([P, PASS_TILES, HALF_TAP_CH * TAPS], F32, name="pool_prod")
+            else:
+                prod = dve_products.tile([P, PASS_TILES, HALF_TAP_CH * TAPS], F32, name="dve_prod")
+            first = tap_channels(t)[0]
+            for group in range(o_lo // GROUP_CH, (o_hi - 1) // GROUP_CH + 1):
+                lo = max(o_lo, group * GROUP_CH)
+                hi = min(o_hi, (group + 1) * GROUP_CH)
                 shape = [P, PASS_TILES, hi - lo, TAPS]
-                nc.vector.tensor_tensor(
-                    out=prod[:, :, (lo - first) * TAPS : (hi - first) * TAPS].rearrange(
-                        "p h (o m) -> p h o m", m=TAPS
+                if t == MIDDLE:
+                    g_part = g_sb[:, tiles, lo:hi]
+                else:
+                    g_part = g_tap[:, tiles, t, lo - first : hi - first]
+                if W_IN_PSUM and not on_pool:
+                    w_part = w_ps[:, tiles, (group - PSUM_GROUP_LO) * TAPS : (group - PSUM_GROUP_LO + 1) * TAPS]
+                else:
+                    w_part = w_sb[:, tiles, group * TAPS : (group + 1) * TAPS]
+                engine = nc.gpsimd if on_pool else nc.vector
+                engine.tensor_tensor(
+                    out=prod[:, :, (lo - o_lo) * TAPS : (hi - o_lo) * TAPS].rearrange(
+                        "p u (o m) -> p u o m", m=TAPS
                     ),
-                    in0=g_sb[:, tiles, lo:hi].unsqueeze(3).to_broadcast(shape),
-                    in1=weights[:, :, group * TAPS : (group + 1) * TAPS]
-                    .unsqueeze(2)
-                    .to_broadcast(shape),
+                    in0=g_part.unsqueeze(3).to_broadcast(shape),
+                    in1=w_part.unsqueeze(2).to_broadcast(shape),
                     op=mybir.AluOpType.mult,
                 )
-            return prod
+            return prod, first_product - o_lo * TAPS
 
-        def add_tap(bank, h, prod, image_in_pass, t):
+        def add_tap(bank, prod, first_col, image_in_pass, t):
             i, j = t // KERNEL, t % KERNEL
-            first_col = t * CH - tap_channels(t)[0] * TAPS
-            for ct in range(h * BANK_CH_TILES, (h + 1) * BANK_CH_TILES):
-                first_in_bank = ct % BANK_CH_TILES == 0
+            for ct in range(BANK_CH_TILES):
                 for half in range(IMAGE_TILES):
                     wanted = half * P + (i - 1) * COLS
                     start_pixel = min(max(wanted, 0), IMAGE_PIXELS - P)
                     turn = (start_pixel - wanted - (j - 1)) % P
                     nc.tensor.matmul(
-                        out=bank[:, ct % BANK_CH_TILES, start_pixel : start_pixel + P],
+                        out=bank[:, ct, start_pixel : start_pixel + P],
                         lhsT=prod[
                             :,
                             image_in_pass * IMAGE_TILES + half,
@@ -171,16 +219,22 @@ def tile_involution2d_pa_s_kernel(tc, x, Wi, bi, w_span, grad_out, out):
                         ],
                         rhs=ident_twice[:, turn : turn + P],
                         is_transpose=True,
-                        start=(t == TAP_ORDER[0] and half == 0 and first_in_bank),
-                        stop=(t == TAP_ORDER[-1] and half == IMAGE_TILES - 1 and not first_in_bank),
+                        start=(t == TAP_ORDER[0] and half == 0 and ct == 0),
+                        stop=(t == TAP_ORDER[-1] and half == IMAGE_TILES - 1 and ct == BANK_CH_TILES - 1),
                     )
 
-        def second_copy(last):
-            return nc.vector.tensor_copy if last else nc.scalar.copy
+        def round_sums(h, sums, gxi_t, last):
+            for image_in_pass in range(PASS_IMAGES):
+                word_rows = slice(image_in_pass * IMAGE_WORD_ROWS, (image_in_pass + 1) * IMAGE_WORD_ROWS)
+                copy_out = nc.vector.tensor_copy if (last and image_in_pass == 1) else nc.scalar.copy
+                copy_out(
+                    out=gxi_t[:, h * BANK_CH_TILES : (h + 1) * BANK_CH_TILES, :, word_rows],
+                    in_=sums[image_in_pass][:].rearrange("c t (a j) -> c t j a", j=PACK),
+                )
 
-        def back_to_pixels(n, gxi_t, gxi_grouped):
-            for h in range(SUM_BANKS):
-                back = back_psum.tile([P, PACK, BANK_CH_TILES * P], BF16, name="back%d" % h)
+        def back_to_pixels(h, gxi_t, gxi_grouped, last):
+            if not last:
+                back = back_psum.tile([P, PACK, HALF_CH], BF16, name="back")
                 for ct in range(BANK_CH_TILES):
                     for j in range(PACK):
                         nc.tensor.transpose(
@@ -188,20 +242,31 @@ def tile_involution2d_pa_s_kernel(tc, x, Wi, bi, w_span, grad_out, out):
                             gxi_t[:, h * BANK_CH_TILES + ct, j, :],
                             ident_bf16[:],
                         )
-                copy_out = nc.scalar.copy if h == 0 else second_copy(n == PASSES - 1)
+                nc.scalar.copy(
+                    out=gxi_grouped[:, h * HALF_CH : (h + 1) * HALF_CH, :],
+                    in_=back[:].rearrange("p j c -> p c j"),
+                )
+                return
+            for ct in range(BANK_CH_TILES):
+                if ct == 0:
+                    back = back_psum.tile([P, PACK, P], BF16, name="back")
+                else:
+                    back = w_psum.tile([P, PACK, P], BF16, name="w_bank")
+                for j in range(PACK):
+                    nc.tensor.transpose(back[:, j, :], gxi_t[:, h * BANK_CH_TILES + ct, j, :], ident_bf16[:])
+                copy_out = nc.scalar.copy if ct == 0 else nc.vector.tensor_copy
                 copy_out(
-                    out=gxi_grouped[:, h * BANK_CH_TILES * P : (h + 1) * BANK_CH_TILES * P, :],
+                    out=gxi_grouped[:, h * HALF_CH + ct * P : h * HALF_CH + (ct + 1) * P, :],
                     in_=back[:].rearrange("p j c -> p c j"),
                 )
 
-        def quantise_gxi(gxi_grouped, gxi_codes, gxi_scales):
-            for h in range(SUM_BANKS):
-                bank_ch = slice(h * BANK_CH_TILES * P, (h + 1) * BANK_CH_TILES * P)
-                nc.vector.quantize_mx(
-                    out=gxi_codes[:, bank_ch].bitcast(E5M2_X4),
-                    scales=gxi_scales[:, bank_ch],
-                    in_=gxi_grouped[:, bank_ch, :].rearrange("p c j -> p (c j)"),
-                )
+        def quantise_gxi(h, gxi_grouped, gxi_codes, gxi_scales):
+            half_ch = slice(h * HALF_CH, (h + 1) * HALF_CH)
+            nc.vector.quantize_mx(
+                out=gxi_codes[:, half_ch].bitcast(E5M2_X4),
+                scales=gxi_scales[:, half_ch],
+                in_=gxi_grouped[:, half_ch, :].rearrange("p c j -> p (c j)"),
+            )
 
         out_acc = [out_psum.tile([P, CH], F32, name="out_acc%d" % m) for m in range(X_CH // P)]
 
@@ -217,54 +282,42 @@ def tile_involution2d_pa_s_kernel(tc, x, Wi, bi, w_span, grad_out, out):
                     stop=(n == PASSES - 1),
                 )
 
-        def finish_stage(stage, n, tiles_of_pass):
-            gxi_t, gxi_grouped, gxi_codes, gxi_scales = tiles_of_pass
-            if stage == 0:
-                back_to_pixels(n, gxi_t, gxi_grouped)
-            elif stage == 1:
-                quantise_gxi(gxi_grouped, gxi_codes, gxi_scales)
-            else:
-                multiply_pass(n, gxi_codes, gxi_scales)
+        later = {}
 
+        def at(phase, step, call):
+            later.setdefault((phase, step), []).append(call)
+
+        phases = [(n, h) for n in range(PASSES) for h in range(HALVES)]
+        LAST = len(phases) - 1
         tiles_of_pass = None
-        for n in range(PASSES):
-            earlier_pass = tiles_of_pass
-            tiles_of_pass = (
-                per_pass.tile([P, CH_TILES, PACK, P], BF16, name="gxi_t"),
-                per_pass.tile([P, CH, PACK], BF16, name="gxi_grouped", align_bytes=64),
-                per_pass.tile([P, CH], U32, name="gxi_codes", align_bytes=64),
-                per_pass.tile([P, CH], U8, name="gxi_scales", align_bytes=64),
-            )
-            sums = [
-                [
-                    sums_psum.tile([P, BANK_CH_TILES, IMAGE_PIXELS], F32, name="sums%d" % h)
-                    for h in range(SUM_BANKS)
-                ]
-                for image_in_pass in range(PASS_IMAGES)
-            ]
+        for phase, (n, h) in enumerate(phases):
+            if h == 0:
+                tiles_of_pass = (
+                    per_pass.tile([P, CH // P, PACK, P], BF16, name="gxi_t"),
+                    per_pass.tile([P, CH, PACK], BF16, name="gxi_grouped", align_bytes=64),
+                    per_pass.tile([P, CH], U32, name="gxi_codes", align_bytes=64),
+                    per_pass.tile([P, CH], U8, name="gxi_scales", align_bytes=64),
+                )
+            gxi_t, gxi_grouped, gxi_codes, gxi_scales = tiles_of_pass
+            sums = [sums_psum.tile([P, BANK_CH_TILES, IMAGE_PIXELS], F32, name="sums") for image in range(PASS_IMAGES)]
             for step, t in enumerate(TAP_ORDER):
-                prod = multiply_tap(n, t)
-                for h in range(SUM_BANKS):
-                    for image_in_pass in range(PASS_IMAGES):
-                        add_tap(sums[image_in_pass][h], h, prod, image_in_pass, t)
-                if earlier_pass is not None and step < FINISH_STAGES:
-                    finish_stage(step, n - 1, earlier_pass)
-            for h in range(SUM_BANKS):
+                prod, first_col = multiply_tap(n, h, t)
                 for image_in_pass in range(PASS_IMAGES):
-                    word_rows = slice(
-                        image_in_pass * IMAGE_WORD_ROWS, (image_in_pass + 1) * IMAGE_WORD_ROWS
-                    )
-                    copy_out = nc.scalar.copy if image_in_pass == 0 else second_copy(n == PASSES - 1)
-                    copy_out(
-                        out=tiles_of_pass[0][
-                            :, h * BANK_CH_TILES : (h + 1) * BANK_CH_TILES, :, word_rows
-                        ],
-                        in_=sums[image_in_pass][h][:].rearrange("c t (a j) -> c t j a", j=PACK),
-                    )
-            if n == 0:
-                quantise_x()
-        for stage in range(FINISH_STAGES):
-            finish_stage(stage, PASSES - 1, tiles_of_pass)
+                    add_tap(sums[image_in_pass], prod, first_col, image_in_pass, t)
+                for call in later.get((phase, step), []):
+                    call()
+            round_sums(h, sums, gxi_t, phase == LAST)
+            if phase == 0:
+                group_x()
+                at(1, TAPS - 1, quantise_x)
+            if phase < LAST:
+                at(phase + 1, 2, lambda h=h, a=gxi_t, b=gxi_grouped: back_to_pixels(h, a, b, False))
+                at(phase + 1, TAPS - 1, lambda h=h, b=gxi_grouped, c=gxi_codes, d=gxi_scales: quantise_gxi(h, b, c, d))
+                if h == HALVES - 1:
+                    at(phase + 2, 2, lambda n=n, c=gxi_codes, d=gxi_scales: multiply_pass(n, c, d))
+        back_to_pixels(HALVES - 1, gxi_t, gxi_grouped, True)
+        quantise_gxi(HALVES - 1, gxi_grouped, gxi_codes, gxi_scales)
+        multiply_pass(PASSES - 1, gxi_codes, gxi_scales)
 
         for m in range(X_CH // P):
             result = keep.tile([P, CH], F32, name="result%d" % m)

@@ -40,7 +40,6 @@ BYTES = 2 * IMAGES * IMAGE_PIXELS * (X_CH + CH + GROUPS * TAPS) + 4 * X_CH * CH
 MIDDLE = 4
 POOL_TAPS = (0, 1, 2)
 TAP_ORDER = (4, 3, 0, 5, 6, 1, 7, 8, 2)
-W_IN_PSUM = len(POOL_TAPS) > 0
 
 
 def tap_channels(t):
@@ -53,9 +52,10 @@ def tap_groups(t):
     return ch_lo // GROUP_CH, (ch_hi - 1) // GROUP_CH + 1
 
 
-PSUM_GROUP_LO = min(tap_groups(t)[0] for t in range(TAPS) if t not in POOL_TAPS)
-PSUM_GROUP_HI = max(tap_groups(t)[1] for t in range(TAPS) if t not in POOL_TAPS)
-PSUM_W = (PSUM_GROUP_HI - PSUM_GROUP_LO) * TAPS
+PSUM_W = 112
+PSUM_W_FIRST = GROUPS * TAPS - PSUM_W
+PSUM_W_BLOCKS = TILES * PSUM_W // P
+KICKS = 3
 
 
 def tile_involution2d_pa_s_kernel(tc, x, Wi, bi, w_span, grad_out, out):
@@ -74,6 +74,8 @@ def tile_involution2d_pa_s_kernel(tc, x, Wi, bi, w_span, grad_out, out):
         w_rows = w_span.rearrange("b h w f -> (b h w) f").rearrange("(u p) f -> p u f", p=P)
         g_sb = keep.tile([P, TILES, CH], BF16)
         w_sb = keep.tile([P, TILES, GROUPS * TAPS], BF16)
+        w_c = keep.tile([P, TILES, PSUM_W], BF16)
+        nc.sync.dma_start(out=w_c[:], in_=w_rows[:, :, PSUM_W_FIRST:])
         nc.sync.dma_start(out=w_sb[:], in_=w_rows)
         for image in range(IMAGES):
             tiles = slice(image * IMAGE_TILES, (image + 1) * IMAGE_TILES)
@@ -94,18 +96,26 @@ def tile_involution2d_pa_s_kernel(tc, x, Wi, bi, w_span, grad_out, out):
         make_identity(nc, ident_twice[:, 0:P])
         make_identity(nc, ident_twice[:, P : 2 * P])
 
-        w_ps = None
-        if W_IN_PSUM:
-            w_ps = w_psum.tile([P, TILES, PSUM_W], BF16, name="w_bank")
-            for n in range(PASSES):
-                tiles = slice(n * PASS_TILES, (n + 1) * PASS_TILES)
+        kick_bank = out_psum.tile([P, P], F32, name="out_acc0")
+
+        def kick():
+            for k in range(KICKS):
                 nc.tensor.matmul(
-                    out=w_ps[:, tiles, :],
-                    lhsT=ident_bf16[:],
-                    rhs=w_sb[:, tiles, PSUM_GROUP_LO * TAPS : PSUM_GROUP_HI * TAPS],
-                    start=True,
-                    stop=True,
+                    out=kick_bank[:], lhsT=ident_twice[:, 0:P], rhs=ident_twice[:, 0:P], start=True, stop=True
                 )
+
+        kick()
+        w_c_flat = w_c[:].rearrange("p u f -> p (u f)")
+        w_t_ps = back_psum.tile([P, PSUM_W_BLOCKS, P], BF16, name="back")
+        for k in range(PSUM_W_BLOCKS):
+            nc.tensor.transpose(w_t_ps[:, k, :], w_c_flat[:, k * P : (k + 1) * P], ident_bf16[:])
+        w_t = keep.tile([P, PSUM_W_BLOCKS, P], BF16)
+        nc.scalar.copy(out=w_t[:], in_=w_t_ps[:])
+        kick()
+        w_ps = w_psum.tile([P, TILES, PSUM_W], BF16, name="w_bank")
+        w_ps_flat = w_ps[:].rearrange("p u f -> p (u f)")
+        for k in range(PSUM_W_BLOCKS):
+            nc.tensor.transpose(w_ps_flat[:, k * P : (k + 1) * P], w_t[:, k, :], ident_bf16[:])
 
         ident_by_col = ident_twice[:, 0:P].rearrange("k (r s) -> k s r", s=COLS)
         on_edge = keep.tile([P, 2], F32)
@@ -169,7 +179,7 @@ def tile_involution2d_pa_s_kernel(tc, x, Wi, bi, w_span, grad_out, out):
                 in_=x_grouped[:].rearrange("p n k j -> p (n k j)"),
             )
 
-        def multiply_tap(n, h, t):
+        def multiply_tap(n, h, t, w_from_sbuf):
             tiles = slice(n * PASS_TILES, (n + 1) * PASS_TILES)
             first_product = t * CH + h * HALF_CH
             o_lo = first_product // TAPS
@@ -188,8 +198,8 @@ def tile_involution2d_pa_s_kernel(tc, x, Wi, bi, w_span, grad_out, out):
                     g_part = g_sb[:, tiles, lo:hi]
                 else:
                     g_part = g_tap[:, tiles, t, lo - first : hi - first]
-                if W_IN_PSUM and not on_pool:
-                    w_part = w_ps[:, tiles, (group - PSUM_GROUP_LO) * TAPS : (group - PSUM_GROUP_LO + 1) * TAPS]
+                if not on_pool and not w_from_sbuf:
+                    w_part = w_ps[:, tiles, group * TAPS - PSUM_W_FIRST : (group + 1) * TAPS - PSUM_W_FIRST]
                 else:
                     w_part = w_sb[:, tiles, group * TAPS : (group + 1) * TAPS]
                 engine = nc.gpsimd if on_pool else nc.vector
@@ -301,7 +311,7 @@ def tile_involution2d_pa_s_kernel(tc, x, Wi, bi, w_span, grad_out, out):
             gxi_t, gxi_grouped, gxi_codes, gxi_scales = tiles_of_pass
             sums = [sums_psum.tile([P, BANK_CH_TILES, IMAGE_PIXELS], F32, name="sums") for image in range(PASS_IMAGES)]
             for step, t in enumerate(TAP_ORDER):
-                prod, first_col = multiply_tap(n, h, t)
+                prod, first_col = multiply_tap(n, h, t, phase == 0 and step < 2)
                 for image_in_pass in range(PASS_IMAGES):
                     add_tap(sums[image_in_pass], prod, first_col, image_in_pass, t)
                 for call in later.get((phase, step), []):

@@ -38,8 +38,8 @@ FLOPS = 2 * IMAGES * IMAGE_PIXELS * X_CH * CH + 2 * IMAGES * IMAGE_PIXELS * CH *
 BYTES = 2 * IMAGES * IMAGE_PIXELS * (X_CH + CH + GROUPS * TAPS) + 4 * X_CH * CH
 
 MIDDLE = 4
-POOL_TAPS = (0, 1, 2)
-TAP_ORDER = (4, 3, 0, 5, 6, 1, 7, 8, 2)
+POOL_TAPS = (0, 1)
+TAP_ORDER = (4, 3, 0, 5, 6, 2, 1, 7, 8)
 
 
 def tap_channels(t):
@@ -198,7 +198,7 @@ def tile_involution2d_pa_s_kernel(tc, x, Wi, bi, w_span, grad_out, out):
                     g_part = g_sb[:, tiles, lo:hi]
                 else:
                     g_part = g_tap[:, tiles, t, lo - first : hi - first]
-                if not on_pool and not w_from_sbuf:
+                if not on_pool and not w_from_sbuf and group * TAPS >= PSUM_W_FIRST:
                     w_part = w_ps[:, tiles, group * TAPS - PSUM_W_FIRST : (group + 1) * TAPS - PSUM_W_FIRST]
                 else:
                     w_part = w_sb[:, tiles, group * TAPS : (group + 1) * TAPS]

@@ -38,8 +38,8 @@ FLOPS = 2 * IMAGES * IMAGE_PIXELS * X_CH * CH + 2 * IMAGES * IMAGE_PIXELS * CH *
 BYTES = 2 * IMAGES * IMAGE_PIXELS * (X_CH + CH + GROUPS * TAPS) + 4 * X_CH * CH
 
 MIDDLE = 4
-POOL_TAPS = (0, 1)
-TAP_ORDER = (4, 3, 0, 5, 6, 2, 1, 7, 8)
+POOL_TAPS = ((0, 1, 2), (0, 1))
+TAP_ORDER = ((4, 3, 0, 5, 6, 1, 7, 8, 2), (4, 3, 5, 0, 6, 7, 1, 8, 2))
 
 
 def tap_channels(t):
@@ -55,7 +55,6 @@ def tap_groups(t):
 PSUM_W = 112
 PSUM_W_FIRST = GROUPS * TAPS - PSUM_W
 PSUM_W_BLOCKS = TILES * PSUM_W // P
-KICKS = 3
 
 
 def tile_involution2d_pa_s_kernel(tc, x, Wi, bi, w_span, grad_out, out):
@@ -63,7 +62,7 @@ def tile_involution2d_pa_s_kernel(tc, x, Wi, bi, w_span, grad_out, out):
     with ExitStack() as ctx:
         keep = ctx.enter_context(tc.tile_pool(name="keep", bufs=1))
         dve_products = ctx.enter_context(tc.tile_pool(name="dve_products", bufs=4))
-        pool_products = ctx.enter_context(tc.tile_pool(name="pool_products", bufs=3))
+        pool_products = ctx.enter_context(tc.tile_pool(name="pool_products", bufs=4))
         per_pass = ctx.enter_context(tc.tile_pool(name="per_pass", bufs=2))
         sums_psum = ctx.enter_context(tc.psum_pool(name="sums_psum", bufs=4))
         back_psum = ctx.enter_context(tc.psum_pool(name="back_psum", bufs=1))
@@ -90,28 +89,18 @@ def tile_involution2d_pa_s_kernel(tc, x, Wi, bi, w_span, grad_out, out):
         nc.vector.memset(warm[:], 0.0)
         nc.scalar.activation(out=warm[:, 1:2], in_=warm[:, 0:1], func=mybir.ActivationFunctionType.Copy)
 
-        ident_bf16 = keep.tile([P, P], BF16)
-        make_identity(nc, ident_bf16[:])
         ident_twice = keep.tile([P, 2 * P], F32)
         make_identity(nc, ident_twice[:, 0:P])
-        make_identity(nc, ident_twice[:, P : 2 * P])
+        ident_bf16 = keep.tile([P, P], BF16)
+        nc.vector.tensor_copy(out=ident_bf16[:], in_=ident_twice[:, 0:P])
+        nc.vector.tensor_copy(out=ident_twice[:, P : 2 * P], in_=ident_twice[:, 0:P])
 
-        kick_bank = out_psum.tile([P, P], F32, name="out_acc0")
-
-        def kick():
-            for k in range(KICKS):
-                nc.tensor.matmul(
-                    out=kick_bank[:], lhsT=ident_twice[:, 0:P], rhs=ident_twice[:, 0:P], start=True, stop=True
-                )
-
-        kick()
         w_c_flat = w_c[:].rearrange("p u f -> p (u f)")
         w_t_ps = back_psum.tile([P, PSUM_W_BLOCKS, P], BF16, name="back")
         for k in range(PSUM_W_BLOCKS):
             nc.tensor.transpose(w_t_ps[:, k, :], w_c_flat[:, k * P : (k + 1) * P], ident_bf16[:])
         w_t = keep.tile([P, PSUM_W_BLOCKS, P], BF16)
         nc.scalar.copy(out=w_t[:], in_=w_t_ps[:])
-        kick()
         w_ps = w_psum.tile([P, TILES, PSUM_W], BF16, name="w_bank")
         w_ps_flat = w_ps[:].rearrange("p u f -> p (u f)")
         for k in range(PSUM_W_BLOCKS):
@@ -147,22 +136,41 @@ def tile_involution2d_pa_s_kernel(tc, x, Wi, bi, w_span, grad_out, out):
         nc.vector.memset(has_neighbour[0:COLS, 0, 0, :], 0.0)
         nc.vector.memset(has_neighbour[P - COLS : P, IMAGE_TILES - 1, KERNEL - 1, :], 0.0)
 
-        g_tap = keep.tile([P, TILES, TAPS, TAP_CH], BF16)
         g_sb_halves = g_sb[:].rearrange("p (b h) f -> p b h f", h=IMAGE_TILES)
-        g_tap_halves = g_tap[:].rearrange("p (b h) t f -> p b h t f", h=IMAGE_TILES)
-        for n in range(PASSES):
+        g_tap = {}
+
+        def mask_g(n):
             images = slice(n * PASS_IMAGES, (n + 1) * PASS_IMAGES)
-            for t in TAP_ORDER:
-                if t == MIDDLE:
+            for t in TAP_ORDER[0]:
+                if t == MIDDLE or all(t in taps for taps in POOL_TAPS):
                     continue
                 first, ch_lo, ch_hi = tap_channels(t)
+                g_tap[(t, n)] = keep.tile([P, PASS_TILES, TAP_CH], BF16, name="g_tap%d_%d" % (t, n))
+                by_half = g_tap[(t, n)][:].rearrange("p (b h) f -> p b h f", h=IMAGE_TILES)
                 for half in range(IMAGE_TILES):
                     nc.scalar.activation(
-                        out=g_tap_halves[:, images, half, t, ch_lo - first : ch_hi - first],
+                        out=by_half[:, :, half, ch_lo - first : ch_hi - first],
                         in_=g_sb_halves[:, images, half, ch_lo:ch_hi],
                         func=mybir.ActivationFunctionType.Copy,
                         scale=has_neighbour[:, half, t // KERNEL, t % KERNEL : t % KERNEL + 1],
                     )
+
+        w_sb_halves = w_sb[:].rearrange("p (b h) f -> p b h f", h=IMAGE_TILES)
+        w_tap = {}
+        for t in TAP_ORDER[0]:
+            if not any(t in taps for taps in POOL_TAPS):
+                continue
+            w_tap[t] = keep.tile([P, TILES, GROUPS * TAPS], BF16, name="w_tap%d" % t)
+            by_half = w_tap[t][:].rearrange("p (b h) f -> p b h f", h=IMAGE_TILES)
+            weights = slice(tap_groups(t)[0] * TAPS, tap_groups(t)[1] * TAPS)
+            for half in range(IMAGE_TILES):
+                nc.scalar.activation(
+                    out=by_half[:, :, half, weights],
+                    in_=w_sb_halves[:, :, half, weights],
+                    func=mybir.ActivationFunctionType.Copy,
+                    scale=has_neighbour[:, half, t // KERNEL, t % KERNEL : t % KERNEL + 1],
+                )
+        mask_g(0)
 
         x_grouped = keep.tile([P, PASSES, X_CH, PACK], BF16, align_bytes=64)
         x_codes = keep.tile([P, PASSES, X_CH], U32, align_bytes=64)
@@ -184,7 +192,7 @@ def tile_involution2d_pa_s_kernel(tc, x, Wi, bi, w_span, grad_out, out):
             first_product = t * CH + h * HALF_CH
             o_lo = first_product // TAPS
             o_hi = (first_product + HALF_CH - 1) // TAPS + 1
-            on_pool = t in POOL_TAPS
+            on_pool = t in POOL_TAPS[h]
             if on_pool:
                 prod = pool_products.tile([P, PASS_TILES, HALF_TAP_CH * TAPS], F32, name="pool_prod")
             else:
@@ -194,14 +202,16 @@ def tile_involution2d_pa_s_kernel(tc, x, Wi, bi, w_span, grad_out, out):
                 lo = max(o_lo, group * GROUP_CH)
                 hi = min(o_hi, (group + 1) * GROUP_CH)
                 shape = [P, PASS_TILES, hi - lo, TAPS]
-                if t == MIDDLE:
+                if t == MIDDLE or on_pool:
                     g_part = g_sb[:, tiles, lo:hi]
                 else:
-                    g_part = g_tap[:, tiles, t, lo - first : hi - first]
-                if not on_pool and not w_from_sbuf and group * TAPS >= PSUM_W_FIRST:
-                    w_part = w_ps[:, tiles, group * TAPS - PSUM_W_FIRST : (group + 1) * TAPS - PSUM_W_FIRST]
-                else:
+                    g_part = g_tap[(t, n)][:, :, lo - first : hi - first]
+                if on_pool:
+                    w_part = w_tap[t][:, tiles, group * TAPS : (group + 1) * TAPS]
+                elif w_from_sbuf:
                     w_part = w_sb[:, tiles, group * TAPS : (group + 1) * TAPS]
+                else:
+                    w_part = w_ps[:, tiles, group * TAPS - PSUM_W_FIRST : (group + 1) * TAPS - PSUM_W_FIRST]
                 engine = nc.gpsimd if on_pool else nc.vector
                 engine.tensor_tensor(
                     out=prod[:, :, (lo - o_lo) * TAPS : (hi - o_lo) * TAPS].rearrange(
@@ -213,7 +223,7 @@ def tile_involution2d_pa_s_kernel(tc, x, Wi, bi, w_span, grad_out, out):
                 )
             return prod, first_product - o_lo * TAPS
 
-        def add_tap(bank, prod, first_col, image_in_pass, t):
+        def add_tap(bank, prod, first_col, image_in_pass, t, first_tap, last_tap):
             i, j = t // KERNEL, t % KERNEL
             for ct in range(BANK_CH_TILES):
                 for half in range(IMAGE_TILES):
@@ -229,8 +239,8 @@ def tile_involution2d_pa_s_kernel(tc, x, Wi, bi, w_span, grad_out, out):
                         ],
                         rhs=ident_twice[:, turn : turn + P],
                         is_transpose=True,
-                        start=(t == TAP_ORDER[0] and half == 0 and ct == 0),
-                        stop=(t == TAP_ORDER[-1] and half == IMAGE_TILES - 1 and ct == BANK_CH_TILES - 1),
+                        start=(first_tap and half == 0 and ct == 0),
+                        stop=(last_tap and half == IMAGE_TILES - 1 and ct == BANK_CH_TILES - 1),
                     )
 
         def round_sums(h, sums, gxi_t, last):
@@ -310,21 +320,22 @@ def tile_involution2d_pa_s_kernel(tc, x, Wi, bi, w_span, grad_out, out):
                 )
             gxi_t, gxi_grouped, gxi_codes, gxi_scales = tiles_of_pass
             sums = [sums_psum.tile([P, BANK_CH_TILES, IMAGE_PIXELS], F32, name="sums") for image in range(PASS_IMAGES)]
-            for step, t in enumerate(TAP_ORDER):
+            for step, t in enumerate(TAP_ORDER[h]):
                 prod, first_col = multiply_tap(n, h, t, phase == 0 and step < 2)
                 for image_in_pass in range(PASS_IMAGES):
-                    add_tap(sums[image_in_pass], prod, first_col, image_in_pass, t)
+                    add_tap(sums[image_in_pass], prod, first_col, image_in_pass, t, step == 0, step == TAPS - 1)
                 for call in later.get((phase, step), []):
                     call()
             round_sums(h, sums, gxi_t, phase == LAST)
             if phase == 0:
+                mask_g(1)
                 group_x()
-                at(1, TAPS - 1, quantise_x)
+                at(LAST, TAPS - 1, quantise_x)
             if phase < LAST:
                 at(phase + 1, 2, lambda h=h, a=gxi_t, b=gxi_grouped: back_to_pixels(h, a, b, False))
-                at(phase + 1, TAPS - 1, lambda h=h, b=gxi_grouped, c=gxi_codes, d=gxi_scales: quantise_gxi(h, b, c, d))
+                at(LAST, TAPS - 1, lambda h=h, b=gxi_grouped, c=gxi_codes, d=gxi_scales: quantise_gxi(h, b, c, d))
                 if h == HALVES - 1:
-                    at(phase + 2, 2, lambda n=n, c=gxi_codes, d=gxi_scales: multiply_pass(n, c, d))
+                    at(LAST, TAPS - 1, lambda n=n, c=gxi_codes, d=gxi_scales: multiply_pass(n, c, d))
         back_to_pixels(HALVES - 1, gxi_t, gxi_grouped, True)
         quantise_gxi(HALVES - 1, gxi_grouped, gxi_codes, gxi_scales)
         multiply_pass(PASSES - 1, gxi_codes, gxi_scales)

@@ -38,6 +38,9 @@ FLOPS = 2 * IMAGES * IMAGE_PIXELS * X_CH * CH + 2 * IMAGES * IMAGE_PIXELS * CH *
 BYTES = 2 * IMAGES * IMAGE_PIXELS * (X_CH + CH + GROUPS * TAPS) + 4 * X_CH * CH
 
 MIDDLE = 4
+LAG = 7
+FIRST_KICKS = 4
+LATER_KICKS = 2
 POOL_TAPS = ((0, 1, 2), (0, 1))
 TAP_ORDER = ((4, 3, 0, 5, 6, 1, 7, 8, 2), (4, 3, 5, 0, 6, 7, 1, 8, 2))
 
@@ -60,9 +63,10 @@ PSUM_W_BLOCKS = TILES * PSUM_W // P
 def tile_involution2d_pa_s_kernel(tc, x, Wi, bi, w_span, grad_out, out):
     nc = tc.nc
     with ExitStack() as ctx:
+        ctx.enter_context(tc.manual_schedule(engines={mybir.EngineType.PE}))
         keep = ctx.enter_context(tc.tile_pool(name="keep", bufs=1))
-        dve_products = ctx.enter_context(tc.tile_pool(name="dve_products", bufs=4))
-        pool_products = ctx.enter_context(tc.tile_pool(name="pool_products", bufs=4))
+        dve_products = ctx.enter_context(tc.tile_pool(name="dve_products", bufs=10))
+        pool_products = ctx.enter_context(tc.tile_pool(name="pool_products", bufs=5))
         per_pass = ctx.enter_context(tc.tile_pool(name="per_pass", bufs=2))
         sums_psum = ctx.enter_context(tc.psum_pool(name="sums_psum", bufs=4))
         back_psum = ctx.enter_context(tc.psum_pool(name="back_psum", bufs=1))
@@ -288,9 +292,11 @@ def tile_involution2d_pa_s_kernel(tc, x, Wi, bi, w_span, grad_out, out):
                 in_=gxi_grouped[:, half_ch, :].rearrange("p c j -> p (c j)"),
             )
 
-        out_acc = [out_psum.tile([P, CH], F32, name="out_acc%d" % m) for m in range(X_CH // P)]
+        out_acc = []
 
         def multiply_pass(n, gxi_codes, gxi_scales):
+            if n == 0:
+                out_acc.extend(out_psum.tile([P, CH], F32, name="out_acc%d" % m) for m in range(X_CH // P))
             for m in range(X_CH // P):
                 nc.tensor.matmul_mx(
                     out=out_acc[m][:],
@@ -309,33 +315,65 @@ def tile_involution2d_pa_s_kernel(tc, x, Wi, bi, w_span, grad_out, out):
 
         phases = [(n, h) for n in range(PASSES) for h in range(HALVES)]
         LAST = len(phases) - 1
-        tiles_of_pass = None
-        for phase, (n, h) in enumerate(phases):
-            if h == 0:
-                tiles_of_pass = (
-                    per_pass.tile([P, CH // P, PACK, P], BF16, name="gxi_t"),
-                    per_pass.tile([P, CH, PACK], BF16, name="gxi_grouped", align_bytes=64),
-                    per_pass.tile([P, CH], U32, name="gxi_codes", align_bytes=64),
-                    per_pass.tile([P, CH], U8, name="gxi_scales", align_bytes=64),
+        steps = [(phase, step) for phase in range(len(phases)) for step in range(TAPS)]
+        made = {}
+        state = {}
+        kick_bank = out_psum.tile([P, P], F32, name="out_acc0")
+
+        def kick(times, prod):
+            for k in range(times):
+                nc.tensor.matmul(
+                    out=kick_bank[:], lhsT=ident_twice[:, 0:P], rhs=prod[:, 0, 0:P], start=True, stop=True
                 )
-            gxi_t, gxi_grouped, gxi_codes, gxi_scales = tiles_of_pass
-            sums = [sums_psum.tile([P, BANK_CH_TILES, IMAGE_PIXELS], F32, name="sums") for image in range(PASS_IMAGES)]
-            for step, t in enumerate(TAP_ORDER[h]):
-                prod, first_col = multiply_tap(n, h, t, phase == 0 and step < 2)
-                for image_in_pass in range(PASS_IMAGES):
-                    add_tap(sums[image_in_pass], prod, first_col, image_in_pass, t, step == 0, step == TAPS - 1)
-                for call in later.get((phase, step), []):
-                    call()
+
+        def produce(phase, step):
+            n, h = phases[phase]
+            made[(phase, step)] = multiply_tap(n, h, TAP_ORDER[h][step], phase == 0 and step < 2)
+
+        def consume(phase, step):
+            n, h = phases[phase]
+            t = TAP_ORDER[h][step]
+            prod, first_col = made[(phase, step)]
+            if step == 0:
+                if h == 0:
+                    state["pass"] = (
+                        per_pass.tile([P, CH // P, PACK, P], BF16, name="gxi_t"),
+                        per_pass.tile([P, CH, PACK], BF16, name="gxi_grouped", align_bytes=64),
+                        per_pass.tile([P, CH], U32, name="gxi_codes", align_bytes=64),
+                        per_pass.tile([P, CH], U8, name="gxi_scales", align_bytes=64),
+                    )
+                state["sums"] = [
+                    sums_psum.tile([P, BANK_CH_TILES, IMAGE_PIXELS], F32, name="sums") for image in range(PASS_IMAGES)
+                ]
+                if phase == 0:
+                    kick(FIRST_KICKS, made[steps[LAG]][0])
+                elif h == 0:
+                    kick(LATER_KICKS, prod)
+            gxi_t, gxi_grouped, gxi_codes, gxi_scales = state["pass"]
+            sums = state["sums"]
+            for image_in_pass in range(PASS_IMAGES):
+                add_tap(sums[image_in_pass], prod, first_col, image_in_pass, t, step == 0, step == TAPS - 1)
+            for call in later.get((phase, step), []):
+                call()
+            if step < TAPS - 1:
+                return
             round_sums(h, sums, gxi_t, phase == LAST)
             if phase == 0:
                 mask_g(1)
                 group_x()
                 at(LAST, TAPS - 1, quantise_x)
             if phase < LAST:
-                at(phase + 1, 2, lambda h=h, a=gxi_t, b=gxi_grouped: back_to_pixels(h, a, b, False))
+                at(phase + 1, 4, lambda h=h, a=gxi_t, b=gxi_grouped: back_to_pixels(h, a, b, False))
                 at(LAST, TAPS - 1, lambda h=h, b=gxi_grouped, c=gxi_codes, d=gxi_scales: quantise_gxi(h, b, c, d))
                 if h == HALVES - 1:
                     at(LAST, TAPS - 1, lambda n=n, c=gxi_codes, d=gxi_scales: multiply_pass(n, c, d))
+
+        for s in range(len(steps) + LAG):
+            if s < len(steps):
+                produce(steps[s][0], steps[s][1])
+            if s >= LAG:
+                consume(steps[s - LAG][0], steps[s - LAG][1])
+        gxi_t, gxi_grouped, gxi_codes, gxi_scales = state["pass"]
         back_to_pixels(HALVES - 1, gxi_t, gxi_grouped, True)
         quantise_gxi(HALVES - 1, gxi_grouped, gxi_codes, gxi_scales)
         multiply_pass(PASSES - 1, gxi_codes, gxi_scales)

@@ -9,6 +9,7 @@ U32 = mybir.dt.uint32
 U8 = mybir.dt.uint8
 E4M3_X4 = mybir.dt.float8_e4m3fn_x4
 E5M2_X4 = mybir.dt.float8_e5m2_x4
+COPY = mybir.ActivationFunctionType.Copy
 
 P = 128
 IMAGES, ROWS, COLS = 4, 8, 32
@@ -32,17 +33,23 @@ PASS_TILES = PASS_IMAGES * IMAGE_TILES
 IMAGE_WORD_ROWS = IMAGE_PIXELS // PACK
 
 TAP_CH = CH // TAPS + 2
-HALF_TAP_CH = HALF_CH // TAPS + 2
+ROW = CH // TAPS + 1
+PLACES = TAPS * ROW
+PROD_W = 528
 
 FLOPS = 2 * IMAGES * IMAGE_PIXELS * X_CH * CH + 2 * IMAGES * IMAGE_PIXELS * CH * TAPS
 BYTES = 2 * IMAGES * IMAGE_PIXELS * (X_CH + CH + GROUPS * TAPS) + 4 * X_CH * CH
 
 MIDDLE = 4
-LAG = 7
-FIRST_KICKS = 4
-LATER_KICKS = 2
-POOL_TAPS = ((0, 1, 2), (0, 1))
-TAP_ORDER = ((4, 3, 0, 5, 6, 1, 7, 8, 2), (4, 3, 5, 0, 6, 7, 1, 8, 2))
+TAP_ORDER = ((4, 0, 3, 5, 1, 2, 6, 8, 7), (4, 1, 3, 0, 5, 2, 6, 8, 7))
+WHO = (("V", "S", "V", "V", "S", "G", "V", "S", "V"), ("V", "G", "V", "S", "V", "G", "V", "S", "V"))
+LAG = 3
+KICKS = (4, 2)
+SBUF_W_STEPS = 2
+
+PSUM_W = 112
+PSUM_W_FIRST = GROUPS * TAPS - PSUM_W
+PSUM_W_BLOCKS = TILES * PSUM_W // P
 
 
 def tap_channels(t):
@@ -55,9 +62,19 @@ def tap_groups(t):
     return ch_lo // GROUP_CH, (ch_hi - 1) // GROUP_CH + 1
 
 
-PSUM_W = 112
-PSUM_W_FIRST = GROUPS * TAPS - PSUM_W
-PSUM_W_BLOCKS = TILES * PSUM_W // P
+def tap_pieces(t):
+    q, m0 = divmod(t * CH, TAPS)
+    runs = [(0, TAPS - m0, m0, q)]
+    if m0:
+        runs.append((TAPS - m0, m0, 0, q + 1))
+    pieces = []
+    for r0, rows, m_first, q_run in runs:
+        end = min(q_run + ROW, CH)
+        for group in range(q_run // GROUP_CH, (end - 1) // GROUP_CH + 1):
+            lo = max(q_run, group * GROUP_CH)
+            hi = min(end, (group + 1) * GROUP_CH)
+            pieces.append((r0, rows, m_first, group, lo - q_run, lo, hi))
+    return pieces
 
 
 def tile_involution2d_pa_s_kernel(tc, x, Wi, bi, w_span, grad_out, out):
@@ -65,25 +82,33 @@ def tile_involution2d_pa_s_kernel(tc, x, Wi, bi, w_span, grad_out, out):
     with ExitStack() as ctx:
         ctx.enter_context(tc.manual_schedule(engines={mybir.EngineType.PE}))
         keep = ctx.enter_context(tc.tile_pool(name="keep", bufs=1))
-        dve_products = ctx.enter_context(tc.tile_pool(name="dve_products", bufs=10))
-        pool_products = ctx.enter_context(tc.tile_pool(name="pool_products", bufs=5))
+        products = {
+            "V": ctx.enter_context(tc.tile_pool(name="v_products", bufs=6)),
+            "G": ctx.enter_context(tc.tile_pool(name="g_products", bufs=3)),
+            "S": ctx.enter_context(tc.tile_pool(name="s_products", bufs=4)),
+        }
         per_pass = ctx.enter_context(tc.tile_pool(name="per_pass", bufs=2))
-        sums_psum = ctx.enter_context(tc.psum_pool(name="sums_psum", bufs=4))
+        sums_psum = ctx.enter_context(tc.psum_pool(name="sums_psum", bufs=6))
         back_psum = ctx.enter_context(tc.psum_pool(name="back_psum", bufs=1))
         w_psum = ctx.enter_context(tc.psum_pool(name="w_psum", bufs=1))
-        out_psum = ctx.enter_context(tc.psum_pool(name="out_psum", bufs=1))
 
         g_rows = grad_out.rearrange("b h w f -> (b h w) f").rearrange("(u p) f -> p u f", p=P)
         w_rows = w_span.rearrange("b h w f -> (b h w) f").rearrange("(u p) f -> p u f", p=P)
         g_sb = keep.tile([P, TILES, CH], BF16)
         w_sb = keep.tile([P, TILES, GROUPS * TAPS], BF16)
         w_c = keep.tile([P, TILES, PSUM_W], BF16)
-        nc.sync.dma_start(out=w_c[:], in_=w_rows[:, :, PSUM_W_FIRST:])
-        nc.sync.dma_start(out=w_sb[:], in_=w_rows)
-        for image in range(IMAGES):
+        x_raw = keep.tile([P, PASSES, PACK, X_CH], BF16)
+
+        def load_g(image):
             tiles = slice(image * IMAGE_TILES, (image + 1) * IMAGE_TILES)
             nc.sync.dma_start(out=g_sb[:, tiles, :], in_=g_rows[:, tiles, :])
-        x_raw = keep.tile([P, PASSES, PACK, X_CH], BF16)
+
+        nc.sync.dma_start(out=w_sb[:], in_=w_rows)
+        load_g(0)
+        load_g(1)
+        nc.sync.dma_start(out=w_c[:], in_=w_rows[:, :, PSUM_W_FIRST:])
+        load_g(2)
+        load_g(3)
         nc.sync.dma_start(
             out=x_raw[:],
             in_=x.rearrange("b h w k -> (b h w) k").rearrange("(n p j) k -> p n j k", p=P, j=PACK),
@@ -91,24 +116,13 @@ def tile_involution2d_pa_s_kernel(tc, x, Wi, bi, w_span, grad_out, out):
 
         warm = keep.tile([P, 2], F32)
         nc.vector.memset(warm[:], 0.0)
-        nc.scalar.activation(out=warm[:, 1:2], in_=warm[:, 0:1], func=mybir.ActivationFunctionType.Copy)
+        nc.scalar.activation(out=warm[:, 1:2], in_=warm[:, 0:1], func=COPY)
 
         ident_twice = keep.tile([P, 2 * P], F32)
         make_identity(nc, ident_twice[:, 0:P])
         ident_bf16 = keep.tile([P, P], BF16)
         nc.vector.tensor_copy(out=ident_bf16[:], in_=ident_twice[:, 0:P])
         nc.vector.tensor_copy(out=ident_twice[:, P : 2 * P], in_=ident_twice[:, 0:P])
-
-        w_c_flat = w_c[:].rearrange("p u f -> p (u f)")
-        w_t_ps = back_psum.tile([P, PSUM_W_BLOCKS, P], BF16, name="back")
-        for k in range(PSUM_W_BLOCKS):
-            nc.tensor.transpose(w_t_ps[:, k, :], w_c_flat[:, k * P : (k + 1) * P], ident_bf16[:])
-        w_t = keep.tile([P, PSUM_W_BLOCKS, P], BF16)
-        nc.scalar.copy(out=w_t[:], in_=w_t_ps[:])
-        w_ps = w_psum.tile([P, TILES, PSUM_W], BF16, name="w_bank")
-        w_ps_flat = w_ps[:].rearrange("p u f -> p (u f)")
-        for k in range(PSUM_W_BLOCKS):
-            nc.tensor.transpose(w_ps_flat[:, k * P : (k + 1) * P], w_t[:, k, :], ident_bf16[:])
 
         ident_by_col = ident_twice[:, 0:P].rearrange("k (r s) -> k s r", s=COLS)
         on_edge = keep.tile([P, 2], F32)
@@ -140,41 +154,46 @@ def tile_involution2d_pa_s_kernel(tc, x, Wi, bi, w_span, grad_out, out):
         nc.vector.memset(has_neighbour[0:COLS, 0, 0, :], 0.0)
         nc.vector.memset(has_neighbour[P - COLS : P, IMAGE_TILES - 1, KERNEL - 1, :], 0.0)
 
-        g_sb_halves = g_sb[:].rearrange("p (b h) f -> p b h f", h=IMAGE_TILES)
-        g_tap = {}
+        def mask_of(t, half):
+            return has_neighbour[:, half, t // KERNEL, t % KERNEL : t % KERNEL + 1]
 
-        def mask_g(n):
+        w_c_flat = w_c[:].rearrange("p u f -> p (u f)")
+        w_t_ps = back_psum.tile([P, PSUM_W_BLOCKS, P], BF16, name="back")
+        for k in range(PSUM_W_BLOCKS):
+            nc.tensor.transpose(w_t_ps[:, k, :], w_c_flat[:, k * P : (k + 1) * P], ident_bf16[:])
+        w_t = keep.tile([P, PSUM_W_BLOCKS, P], BF16)
+        nc.scalar.copy(out=w_t[:], in_=w_t_ps[:])
+        w_ps = w_psum.tile([P, TILES, PSUM_W], BF16, name="w_bank")
+        w_ps_flat = w_ps[:].rearrange("p u f -> p (u f)")
+        for k in range(PSUM_W_BLOCKS):
+            nc.tensor.transpose(w_ps_flat[:, k * P : (k + 1) * P], w_t[:, k, :], ident_bf16[:])
+
+        g_sb_halves = g_sb[:].rearrange("p (b h) f -> p b h f", h=IMAGE_TILES)
+        w_sb_halves = w_sb[:].rearrange("p (b h) f -> p b h f", h=IMAGE_TILES)
+        masked = {}
+
+        def make_masks(n):
             images = slice(n * PASS_IMAGES, (n + 1) * PASS_IMAGES)
-            for t in TAP_ORDER[0]:
-                if t == MIDDLE or all(t in taps for taps in POOL_TAPS):
-                    continue
-                first, ch_lo, ch_hi = tap_channels(t)
-                g_tap[(t, n)] = keep.tile([P, PASS_TILES, TAP_CH], BF16, name="g_tap%d_%d" % (t, n))
-                by_half = g_tap[(t, n)][:].rearrange("p (b h) f -> p b h f", h=IMAGE_TILES)
+            for t, who in zip(TAP_ORDER[n], WHO[n]):
+                if who == "V":
+                    if t == MIDDLE:
+                        continue
+                    first, ch_lo, ch_hi = tap_channels(t)
+                    masked[(t, n)] = keep.tile([P, PASS_TILES, TAP_CH], BF16, name="g_tap%d_%d" % (t, n))
+                    src, cols_in, cols_out = g_sb_halves, slice(ch_lo, ch_hi), slice(ch_lo - first, ch_hi - first)
+                else:
+                    dtype = BF16 if who == "G" else F32
+                    masked[(t, n)] = keep.tile([P, PASS_TILES, GROUPS * TAPS], dtype, name="w_tap%d_%d" % (t, n))
+                    cols_in = slice(tap_groups(t)[0] * TAPS, tap_groups(t)[1] * TAPS)
+                    src, cols_out = w_sb_halves, cols_in
+                by_half = masked[(t, n)][:].rearrange("p (b h) f -> p b h f", h=IMAGE_TILES)
                 for half in range(IMAGE_TILES):
                     nc.scalar.activation(
-                        out=by_half[:, :, half, ch_lo - first : ch_hi - first],
-                        in_=g_sb_halves[:, images, half, ch_lo:ch_hi],
-                        func=mybir.ActivationFunctionType.Copy,
-                        scale=has_neighbour[:, half, t // KERNEL, t % KERNEL : t % KERNEL + 1],
+                        out=by_half[:, :, half, cols_out],
+                        in_=src[:, images, half, cols_in],
+                        func=COPY,
+                        scale=mask_of(t, half),
                     )
-
-        w_sb_halves = w_sb[:].rearrange("p (b h) f -> p b h f", h=IMAGE_TILES)
-        w_tap = {}
-        for t in TAP_ORDER[0]:
-            if not any(t in taps for taps in POOL_TAPS):
-                continue
-            w_tap[t] = keep.tile([P, TILES, GROUPS * TAPS], BF16, name="w_tap%d" % t)
-            by_half = w_tap[t][:].rearrange("p (b h) f -> p b h f", h=IMAGE_TILES)
-            weights = slice(tap_groups(t)[0] * TAPS, tap_groups(t)[1] * TAPS)
-            for half in range(IMAGE_TILES):
-                nc.scalar.activation(
-                    out=by_half[:, :, half, weights],
-                    in_=w_sb_halves[:, :, half, weights],
-                    func=mybir.ActivationFunctionType.Copy,
-                    scale=has_neighbour[:, half, t // KERNEL, t % KERNEL : t % KERNEL + 1],
-                )
-        mask_g(0)
 
         x_grouped = keep.tile([P, PASSES, X_CH, PACK], BF16, align_bytes=64)
         x_codes = keep.tile([P, PASSES, X_CH], U32, align_bytes=64)
@@ -191,56 +210,52 @@ def tile_involution2d_pa_s_kernel(tc, x, Wi, bi, w_span, grad_out, out):
                 in_=x_grouped[:].rearrange("p n k j -> p (n k j)"),
             )
 
-        def multiply_tap(n, h, t, w_from_sbuf):
+        def multiply_tap(n, t, who, w_from_sbuf):
             tiles = slice(n * PASS_TILES, (n + 1) * PASS_TILES)
-            first_product = t * CH + h * HALF_CH
-            o_lo = first_product // TAPS
-            o_hi = (first_product + HALF_CH - 1) // TAPS + 1
-            on_pool = t in POOL_TAPS[h]
-            if on_pool:
-                prod = pool_products.tile([P, PASS_TILES, HALF_TAP_CH * TAPS], F32, name="pool_prod")
-            else:
-                prod = dve_products.tile([P, PASS_TILES, HALF_TAP_CH * TAPS], F32, name="dve_prod")
+            prod = products[who].tile([P, PASS_TILES, PROD_W], F32, name="prod_" + who)
+            by_row = prod[:, :, 0:PLACES].rearrange("p u (r i) -> p u r i", i=ROW)
             first = tap_channels(t)[0]
-            for group in range(o_lo // GROUP_CH, (o_hi - 1) // GROUP_CH + 1):
-                lo = max(o_lo, group * GROUP_CH)
-                hi = min(o_hi, (group + 1) * GROUP_CH)
-                shape = [P, PASS_TILES, hi - lo, TAPS]
-                if t == MIDDLE or on_pool:
-                    g_part = g_sb[:, tiles, lo:hi]
+            for r0, rows, m_first, group, i0, lo, hi in tap_pieces(t):
+                weights = slice(group * TAPS + m_first, group * TAPS + m_first + rows)
+                if who == "S":
+                    for u in range(PASS_TILES):
+                        for k in range(rows):
+                            nc.scalar.activation(
+                                out=by_row[:, u, r0 + k, i0 : i0 + hi - lo],
+                                in_=g_sb[:, n * PASS_TILES + u, lo:hi],
+                                func=COPY,
+                                scale=masked[(t, n)][:, u, weights.start + k : weights.start + k + 1],
+                            )
+                    continue
+                shape = [P, PASS_TILES, rows, hi - lo]
+                if who == "G":
+                    engine, g_part, w_part = nc.gpsimd, g_sb[:, tiles, lo:hi], masked[(t, n)][:, :, weights]
                 else:
-                    g_part = g_tap[(t, n)][:, :, lo - first : hi - first]
-                if on_pool:
-                    w_part = w_tap[t][:, tiles, group * TAPS : (group + 1) * TAPS]
-                elif w_from_sbuf:
-                    w_part = w_sb[:, tiles, group * TAPS : (group + 1) * TAPS]
-                else:
-                    w_part = w_ps[:, tiles, group * TAPS - PSUM_W_FIRST : (group + 1) * TAPS - PSUM_W_FIRST]
-                engine = nc.gpsimd if on_pool else nc.vector
+                    engine = nc.vector
+                    g_part = g_sb[:, tiles, lo:hi] if t == MIDDLE else masked[(t, n)][:, :, lo - first : hi - first]
+                    if w_from_sbuf:
+                        w_part = w_sb[:, tiles, weights]
+                    else:
+                        w_part = w_ps[:, tiles, weights.start - PSUM_W_FIRST : weights.stop - PSUM_W_FIRST]
                 engine.tensor_tensor(
-                    out=prod[:, :, (lo - o_lo) * TAPS : (hi - o_lo) * TAPS].rearrange(
-                        "p u (o m) -> p u o m", m=TAPS
-                    ),
-                    in0=g_part.unsqueeze(3).to_broadcast(shape),
-                    in1=w_part.unsqueeze(2).to_broadcast(shape),
+                    out=by_row[:, :, r0 : r0 + rows, i0 : i0 + hi - lo],
+                    in0=g_part.unsqueeze(2).to_broadcast(shape),
+                    in1=w_part.unsqueeze(3).to_broadcast(shape),
                     op=mybir.AluOpType.mult,
                 )
-            return prod, first_product - o_lo * TAPS
+            return prod
 
-        def add_tap(bank, prod, first_col, image_in_pass, t, first_tap, last_tap):
+        def add_tap(bank, h, prod, image_in_pass, t, first_tap, last_tap):
             i, j = t // KERNEL, t % KERNEL
             for ct in range(BANK_CH_TILES):
                 for half in range(IMAGE_TILES):
                     wanted = half * P + (i - 1) * COLS
                     start_pixel = min(max(wanted, 0), IMAGE_PIXELS - P)
                     turn = (start_pixel - wanted - (j - 1)) % P
+                    place = (h * BANK_CH_TILES + ct) * P
                     nc.tensor.matmul(
                         out=bank[:, ct, start_pixel : start_pixel + P],
-                        lhsT=prod[
-                            :,
-                            image_in_pass * IMAGE_TILES + half,
-                            first_col + ct * P : first_col + (ct + 1) * P,
-                        ],
+                        lhsT=prod[:, image_in_pass * IMAGE_TILES + half, place : place + P],
                         rhs=ident_twice[:, turn : turn + P],
                         is_transpose=True,
                         start=(first_tap and half == 0 and ct == 0),
@@ -253,36 +268,24 @@ def tile_involution2d_pa_s_kernel(tc, x, Wi, bi, w_span, grad_out, out):
                 copy_out = nc.vector.tensor_copy if (last and image_in_pass == 1) else nc.scalar.copy
                 copy_out(
                     out=gxi_t[:, h * BANK_CH_TILES : (h + 1) * BANK_CH_TILES, :, word_rows],
-                    in_=sums[image_in_pass][:].rearrange("c t (a j) -> c t j a", j=PACK),
+                    in_=sums[image_in_pass][h][:].rearrange("c t (a j) -> c t j a", j=PACK),
                 )
 
         def back_to_pixels(h, gxi_t, gxi_grouped, last):
-            if not last:
+            if last and h == 1:
+                back = w_psum.tile([P, PACK, HALF_CH], BF16, name="w_bank")
+            else:
                 back = back_psum.tile([P, PACK, HALF_CH], BF16, name="back")
-                for ct in range(BANK_CH_TILES):
-                    for j in range(PACK):
-                        nc.tensor.transpose(
-                            back[:, j, ct * P : (ct + 1) * P],
-                            gxi_t[:, h * BANK_CH_TILES + ct, j, :],
-                            ident_bf16[:],
-                        )
-                nc.scalar.copy(
-                    out=gxi_grouped[:, h * HALF_CH : (h + 1) * HALF_CH, :],
-                    in_=back[:].rearrange("p j c -> p c j"),
-                )
-                return
             for ct in range(BANK_CH_TILES):
-                if ct == 0:
-                    back = back_psum.tile([P, PACK, P], BF16, name="back")
-                else:
-                    back = w_psum.tile([P, PACK, P], BF16, name="w_bank")
                 for j in range(PACK):
-                    nc.tensor.transpose(back[:, j, :], gxi_t[:, h * BANK_CH_TILES + ct, j, :], ident_bf16[:])
-                copy_out = nc.scalar.copy if ct == 0 else nc.vector.tensor_copy
-                copy_out(
-                    out=gxi_grouped[:, h * HALF_CH + ct * P : h * HALF_CH + (ct + 1) * P, :],
-                    in_=back[:].rearrange("p j c -> p c j"),
-                )
+                    nc.tensor.transpose(
+                        back[:, j, ct * P : (ct + 1) * P], gxi_t[:, h * BANK_CH_TILES + ct, j, :], ident_bf16[:]
+                    )
+            copy_out = nc.vector.tensor_copy if (last and h == 1) else nc.scalar.copy
+            copy_out(
+                out=gxi_grouped[:, h * HALF_CH : (h + 1) * HALF_CH, :],
+                in_=back[:].rearrange("p j c -> p c j"),
+            )
 
         def quantise_gxi(h, gxi_grouped, gxi_codes, gxi_scales):
             half_ch = slice(h * HALF_CH, (h + 1) * HALF_CH)
@@ -296,7 +299,7 @@ def tile_involution2d_pa_s_kernel(tc, x, Wi, bi, w_span, grad_out, out):
 
         def multiply_pass(n, gxi_codes, gxi_scales):
             if n == 0:
-                out_acc.extend(out_psum.tile([P, CH], F32, name="out_acc%d" % m) for m in range(X_CH // P))
+                out_acc.extend(sums_psum.tile([P, CH], F32, name="sums") for m in range(X_CH // P))
             for m in range(X_CH // P):
                 nc.tensor.matmul_mx(
                     out=out_acc[m][:],
@@ -310,79 +313,80 @@ def tile_involution2d_pa_s_kernel(tc, x, Wi, bi, w_span, grad_out, out):
 
         later = {}
 
-        def at(phase, step, call):
-            later.setdefault((phase, step), []).append(call)
+        def at(n, step, call):
+            later.setdefault((n, step), []).append(call)
 
-        phases = [(n, h) for n in range(PASSES) for h in range(HALVES)]
-        LAST = len(phases) - 1
-        steps = [(phase, step) for phase in range(len(phases)) for step in range(TAPS)]
+        steps = [(n, step) for n in range(PASSES) for step in range(TAPS)]
         made = {}
         state = {}
-        kick_bank = out_psum.tile([P, P], F32, name="out_acc0")
 
         def kick(times, prod):
+            kick_bank = back_psum.tile([P, P], F32, name="back")
             for k in range(times):
                 nc.tensor.matmul(
                     out=kick_bank[:], lhsT=ident_twice[:, 0:P], rhs=prod[:, 0, 0:P], start=True, stop=True
                 )
 
-        def produce(phase, step):
-            n, h = phases[phase]
-            made[(phase, step)] = multiply_tap(n, h, TAP_ORDER[h][step], phase == 0 and step < 2)
-
-        def consume(phase, step):
-            n, h = phases[phase]
-            t = TAP_ORDER[h][step]
-            prod, first_col = made[(phase, step)]
+        def consume(n, step):
+            t = TAP_ORDER[n][step]
+            prod = made[(n, step)]
+            last = n == PASSES - 1
             if step == 0:
-                if h == 0:
-                    state["pass"] = (
-                        per_pass.tile([P, CH // P, PACK, P], BF16, name="gxi_t"),
-                        per_pass.tile([P, CH, PACK], BF16, name="gxi_grouped", align_bytes=64),
-                        per_pass.tile([P, CH], U32, name="gxi_codes", align_bytes=64),
-                        per_pass.tile([P, CH], U8, name="gxi_scales", align_bytes=64),
-                    )
-                state["sums"] = [
-                    sums_psum.tile([P, BANK_CH_TILES, IMAGE_PIXELS], F32, name="sums") for image in range(PASS_IMAGES)
+                state["pass"] = (
+                    per_pass.tile([P, CH // P, PACK, P], BF16, name="gxi_t"),
+                    per_pass.tile([P, CH, PACK], BF16, name="gxi_grouped", align_bytes=64),
+                    per_pass.tile([P, CH], U32, name="gxi_codes", align_bytes=64),
+                    per_pass.tile([P, CH], U8, name="gxi_scales", align_bytes=64),
+                )
+                by_bank = [
+                    sums_psum.tile([P, BANK_CH_TILES, IMAGE_PIXELS], F32, name="sums")
+                    for k in range(HALVES * PASS_IMAGES)
                 ]
-                if phase == 0:
-                    kick(FIRST_KICKS, made[steps[LAG]][0])
-                elif h == 0:
-                    kick(LATER_KICKS, prod)
+                state["sums"] = [[by_bank[h * PASS_IMAGES + image] for h in range(HALVES)] for image in range(PASS_IMAGES)]
+                kick(KICKS[n], made[steps[LAG]] if n == 0 else prod)
             gxi_t, gxi_grouped, gxi_codes, gxi_scales = state["pass"]
             sums = state["sums"]
-            for image_in_pass in range(PASS_IMAGES):
-                add_tap(sums[image_in_pass], prod, first_col, image_in_pass, t, step == 0, step == TAPS - 1)
-            for call in later.get((phase, step), []):
+            for h in range(HALVES):
+                for image_in_pass in range(PASS_IMAGES):
+                    add_tap(sums[image_in_pass][h], h, prod, image_in_pass, t, step == 0, step == TAPS - 1)
+                if step == TAPS - 1:
+                    round_sums(h, sums, gxi_t, last)
+            for call in later.get((n, step), []):
                 call()
-            if step < TAPS - 1:
-                return
-            round_sums(h, sums, gxi_t, phase == LAST)
-            if phase == 0:
-                mask_g(1)
-                group_x()
-                at(LAST, TAPS - 1, quantise_x)
-            if phase < LAST:
-                at(phase + 1, 4, lambda h=h, a=gxi_t, b=gxi_grouped: back_to_pixels(h, a, b, False))
-                at(LAST, TAPS - 1, lambda h=h, b=gxi_grouped, c=gxi_codes, d=gxi_scales: quantise_gxi(h, b, c, d))
-                if h == HALVES - 1:
-                    at(LAST, TAPS - 1, lambda n=n, c=gxi_codes, d=gxi_scales: multiply_pass(n, c, d))
+            if step == TAPS - 1 and not last:
+                at(n + 1, 2, lambda a=gxi_t, b=gxi_grouped: back_to_pixels(0, a, b, False))
+                at(n + 1, 4, lambda a=gxi_t, b=gxi_grouped: back_to_pixels(1, a, b, False))
+                at(n + 1, TAPS - 1, quantise_x)
+                for h in range(HALVES):
+                    at(n + 1, TAPS - 1, lambda h=h, b=gxi_grouped, c=gxi_codes, d=gxi_scales: quantise_gxi(h, b, c, d))
+                at(n + 1, TAPS - 1, lambda n=n, c=gxi_codes, d=gxi_scales: multiply_pass(n, c, d))
 
+        make_masks(0)
         for s in range(len(steps) + LAG):
+            if s == 6:
+                make_masks(1)
+            if s == 9:
+                group_x()
             if s < len(steps):
-                produce(steps[s][0], steps[s][1])
+                n, step = steps[s]
+                made[(n, step)] = multiply_tap(n, TAP_ORDER[n][step], WHO[n][step], s < SBUF_W_STEPS)
             if s >= LAG:
                 consume(steps[s - LAG][0], steps[s - LAG][1])
         gxi_t, gxi_grouped, gxi_codes, gxi_scales = state["pass"]
-        back_to_pixels(HALVES - 1, gxi_t, gxi_grouped, True)
-        quantise_gxi(HALVES - 1, gxi_grouped, gxi_codes, gxi_scales)
+        for h in range(HALVES):
+            back_to_pixels(h, gxi_t, gxi_grouped, True)
+        for h in range(HALVES):
+            quantise_gxi(h, gxi_grouped, gxi_codes, gxi_scales)
         multiply_pass(PASSES - 1, gxi_codes, gxi_scales)
 
         for m in range(X_CH // P):
-            result = keep.tile([P, CH], F32, name="result%d" % m)
-            if m % 2 == 0:
-                nc.scalar.copy(out=result[:], in_=out_acc[m][:])
-                nc.scalar.dma_start(out=out[m * P : (m + 1) * P, :], in_=result[:])
-            else:
-                nc.vector.tensor_copy(out=result[:], in_=out_acc[m][:])
-                nc.sync.dma_start(out=out[m * P : (m + 1) * P, :], in_=result[:])
+            result = keep.tile([P, PLACES], F32, name="result%d" % m)
+            by_channel = result[:].rearrange("p (i r) -> p i r", r=TAPS)
+            copy_out = nc.scalar.copy if m % 2 == 0 else nc.vector.tensor_copy
+            queue = nc.scalar if m % 2 == 0 else nc.sync
+            copy_out(
+                out=by_channel[:, :, 0 : TAPS - 1],
+                in_=out_acc[m][:, 0 : (TAPS - 1) * ROW].rearrange("p (r i) -> p i r", i=ROW),
+            )
+            copy_out(out=by_channel[:, 0 : ROW - 1, TAPS - 1], in_=out_acc[m][:, (TAPS - 1) * ROW : CH])
+            queue.dma_start(out=out[m * P : (m + 1) * P, :], in_=result[:, 0:CH])

@@ -41,13 +41,13 @@ FLOPS = 2 * IMAGES * IMAGE_PIXELS * X_CH * CH + 2 * IMAGES * IMAGE_PIXELS * CH *
 BYTES = 2 * IMAGES * IMAGE_PIXELS * (X_CH + CH + GROUPS * TAPS) + 4 * X_CH * CH
 
 MIDDLE = 4
-TAP_ORDER = ((4, 0, 3, 5, 1, 2, 6, 8, 7), (4, 1, 3, 0, 5, 2, 6, 8, 7))
-WHO = (("V", "S", "V", "V", "S", "G", "V", "S", "V"), ("V", "G", "V", "S", "V", "G", "V", "S", "V"))
+TAP_ORDER = ((4, 3, 0, 5, 2, 1, 8, 6, 7), (4, 1, 3, 0, 8, 5, 6, 2, 7))
+WHO = (("V", "V", "S", "V", "V", "G", "S", "V", "V"), ("V", "G", "V", "S", "G", "V", "V", "G", "V"))
 LAG = 3
 KICKS = (4, 2)
 SBUF_W_STEPS = 2
 
-PSUM_W = 112
+PSUM_W = 128
 PSUM_W_FIRST = GROUPS * TAPS - PSUM_W
 PSUM_W_BLOCKS = TILES * PSUM_W // P
 
@@ -85,7 +85,7 @@ def tile_involution2d_pa_s_kernel(tc, x, Wi, bi, w_span, grad_out, out):
         products = {
             "V": ctx.enter_context(tc.tile_pool(name="v_products", bufs=6)),
             "G": ctx.enter_context(tc.tile_pool(name="g_products", bufs=3)),
-            "S": ctx.enter_context(tc.tile_pool(name="s_products", bufs=4)),
+            "S": ctx.enter_context(tc.tile_pool(name="s_products", bufs=3)),
         }
         per_pass = ctx.enter_context(tc.tile_pool(name="per_pass", bufs=2))
         sums_psum = ctx.enter_context(tc.psum_pool(name="sums_psum", bufs=6))

@@ -41,8 +41,8 @@ FLOPS = 2 * IMAGES * IMAGE_PIXELS * X_CH * CH + 2 * IMAGES * IMAGE_PIXELS * CH *
 BYTES = 2 * IMAGES * IMAGE_PIXELS * (X_CH + CH + GROUPS * TAPS) + 4 * X_CH * CH
 
 MIDDLE = 4
-TAP_ORDER = ((4, 3, 0, 5, 2, 1, 8, 6, 7), (4, 1, 3, 0, 8, 5, 6, 2, 7))
-WHO = (("V", "V", "S", "V", "V", "G", "S", "V", "V"), ("V", "G", "V", "S", "G", "V", "V", "G", "V"))
+TAP_ORDER = ((4, 3, 0, 5, 2, 1, 8, 6, 7), (4, 1, 3, 0, 5, 2, 6, 8, 7))
+WHO = (("V", "V", "S", "V", "V", "G", "S", "V", "V"), ("V", "G", "V", "S", "V", "G", "V", "VG", "V"))
 LAG = 3
 KICKS = (4, 2)
 SBUF_W_STEPS = 2
@@ -86,6 +86,7 @@ def tile_involution2d_pa_s_kernel(tc, x, Wi, bi, w_span, grad_out, out):
             "V": ctx.enter_context(tc.tile_pool(name="v_products", bufs=6)),
             "G": ctx.enter_context(tc.tile_pool(name="g_products", bufs=3)),
             "S": ctx.enter_context(tc.tile_pool(name="s_products", bufs=3)),
+            "VG": ctx.enter_context(tc.tile_pool(name="vg_products", bufs=1)),
         }
         per_pass = ctx.enter_context(tc.tile_pool(name="per_pass", bufs=2))
         sums_psum = ctx.enter_context(tc.psum_pool(name="sums_psum", bufs=6))
@@ -174,19 +175,19 @@ def tile_involution2d_pa_s_kernel(tc, x, Wi, bi, w_span, grad_out, out):
 
         def make_masks(n):
             images = slice(n * PASS_IMAGES, (n + 1) * PASS_IMAGES)
-            for t, who in zip(TAP_ORDER[n], WHO[n]):
+            for t, who in [(t, who) for t, whos in zip(TAP_ORDER[n], WHO[n]) for who in sorted(set(whos))]:
                 if who == "V":
                     if t == MIDDLE:
                         continue
                     first, ch_lo, ch_hi = tap_channels(t)
-                    masked[(t, n)] = keep.tile([P, PASS_TILES, TAP_CH], BF16, name="g_tap%d_%d" % (t, n))
+                    masked[(t, n, who)] = keep.tile([P, PASS_TILES, TAP_CH], BF16, name="g_tap%d_%d" % (t, n))
                     src, cols_in, cols_out = g_sb_halves, slice(ch_lo, ch_hi), slice(ch_lo - first, ch_hi - first)
                 else:
                     dtype = BF16 if who == "G" else F32
-                    masked[(t, n)] = keep.tile([P, PASS_TILES, GROUPS * TAPS], dtype, name="w_tap%d_%d" % (t, n))
+                    masked[(t, n, who)] = keep.tile([P, PASS_TILES, GROUPS * TAPS], dtype, name="w_tap%d_%d" % (t, n))
                     cols_in = slice(tap_groups(t)[0] * TAPS, tap_groups(t)[1] * TAPS)
                     src, cols_out = w_sb_halves, cols_in
-                by_half = masked[(t, n)][:].rearrange("p (b h) f -> p b h f", h=IMAGE_TILES)
+                by_half = masked[(t, n, who)][:].rearrange("p (b h) f -> p b h f", h=IMAGE_TILES)
                 for half in range(IMAGE_TILES):
                     nc.scalar.activation(
                         out=by_half[:, :, half, cols_out],
@@ -210,39 +211,45 @@ def tile_involution2d_pa_s_kernel(tc, x, Wi, bi, w_span, grad_out, out):
                 in_=x_grouped[:].rearrange("p n k j -> p (n k j)"),
             )
 
-        def multiply_tap(n, t, who, w_from_sbuf):
-            tiles = slice(n * PASS_TILES, (n + 1) * PASS_TILES)
-            prod = products[who].tile([P, PASS_TILES, PROD_W], F32, name="prod_" + who)
+        def multiply_tap(n, t, whos, w_from_sbuf):
+            prod = products[whos].tile([P, PASS_TILES, PROD_W], F32, name="prod_" + whos)
             by_row = prod[:, :, 0:PLACES].rearrange("p u (r i) -> p u r i", i=ROW)
             first = tap_channels(t)[0]
-            for r0, rows, m_first, group, i0, lo, hi in tap_pieces(t):
-                weights = slice(group * TAPS + m_first, group * TAPS + m_first + rows)
-                if who == "S":
-                    for u in range(PASS_TILES):
-                        for k in range(rows):
-                            nc.scalar.activation(
-                                out=by_row[:, u, r0 + k, i0 : i0 + hi - lo],
-                                in_=g_sb[:, n * PASS_TILES + u, lo:hi],
-                                func=COPY,
-                                scale=masked[(t, n)][:, u, weights.start + k : weights.start + k + 1],
-                            )
-                    continue
-                shape = [P, PASS_TILES, rows, hi - lo]
-                if who == "G":
-                    engine, g_part, w_part = nc.gpsimd, g_sb[:, tiles, lo:hi], masked[(t, n)][:, :, weights]
-                else:
-                    engine = nc.vector
-                    g_part = g_sb[:, tiles, lo:hi] if t == MIDDLE else masked[(t, n)][:, :, lo - first : hi - first]
-                    if w_from_sbuf:
-                        w_part = w_sb[:, tiles, weights]
+            share = PASS_TILES // len(whos)
+            for k_who, who in enumerate(whos):
+                mine = slice(k_who * share, (k_who + 1) * share)
+                tiles = slice(n * PASS_TILES + mine.start, n * PASS_TILES + mine.stop)
+                for r0, rows, m_first, group, i0, lo, hi in tap_pieces(t):
+                    weights = slice(group * TAPS + m_first, group * TAPS + m_first + rows)
+                    if who == "S":
+                        for u in range(mine.start, mine.stop):
+                            for k in range(rows):
+                                nc.scalar.activation(
+                                    out=by_row[:, u, r0 + k, i0 : i0 + hi - lo],
+                                    in_=g_sb[:, n * PASS_TILES + u, lo:hi],
+                                    func=COPY,
+                                    scale=masked[(t, n, who)][:, u, weights.start + k : weights.start + k + 1],
+                                )
+                        continue
+                    shape = [P, share, rows, hi - lo]
+                    if who == "G":
+                        engine, g_part, w_part = nc.gpsimd, g_sb[:, tiles, lo:hi], masked[(t, n, who)][:, mine, weights]
                     else:
-                        w_part = w_ps[:, tiles, weights.start - PSUM_W_FIRST : weights.stop - PSUM_W_FIRST]
-                engine.tensor_tensor(
-                    out=by_row[:, :, r0 : r0 + rows, i0 : i0 + hi - lo],
-                    in0=g_part.unsqueeze(2).to_broadcast(shape),
-                    in1=w_part.unsqueeze(3).to_broadcast(shape),
-                    op=mybir.AluOpType.mult,
-                )
+                        engine = nc.vector
+                        if t == MIDDLE:
+                            g_part = g_sb[:, tiles, lo:hi]
+                        else:
+                            g_part = masked[(t, n, who)][:, mine, lo - first : hi - first]
+                        if w_from_sbuf:
+                            w_part = w_sb[:, tiles, weights]
+                        else:
+                            w_part = w_ps[:, tiles, weights.start - PSUM_W_FIRST : weights.stop - PSUM_W_FIRST]
+                    engine.tensor_tensor(
+                        out=by_row[:, mine, r0 : r0 + rows, i0 : i0 + hi - lo],
+                        in0=g_part.unsqueeze(2).to_broadcast(shape),
+                        in1=w_part.unsqueeze(3).to_broadcast(shape),
+                        op=mybir.AluOpType.mult,
+                    )
             return prod
 
         def add_tap(bank, h, prod, image_in_pass, t, first_tap, last_tap):
@@ -354,12 +361,10 @@ def tile_involution2d_pa_s_kernel(tc, x, Wi, bi, w_span, grad_out, out):
             for call in later.get((n, step), []):
                 call()
             if step == TAPS - 1 and not last:
-                at(n + 1, 2, lambda a=gxi_t, b=gxi_grouped: back_to_pixels(0, a, b, False))
-                at(n + 1, 4, lambda a=gxi_t, b=gxi_grouped: back_to_pixels(1, a, b, False))
-                at(n + 1, TAPS - 1, quantise_x)
-                for h in range(HALVES):
-                    at(n + 1, TAPS - 1, lambda h=h, b=gxi_grouped, c=gxi_codes, d=gxi_scales: quantise_gxi(h, b, c, d))
-                at(n + 1, TAPS - 1, lambda n=n, c=gxi_codes, d=gxi_scales: multiply_pass(n, c, d))
+                at(n + 1, 0, lambda a=gxi_t, b=gxi_grouped: back_to_pixels(0, a, b, False))
+                at(n + 1, 2, lambda a=gxi_t, b=gxi_grouped: back_to_pixels(1, a, b, False))
+                state["earlier"] = state["pass"]
+
 
         make_masks(0)
         for s in range(len(steps) + LAG):
@@ -370,11 +375,16 @@ def tile_involution2d_pa_s_kernel(tc, x, Wi, bi, w_span, grad_out, out):
             if s < len(steps):
                 n, step = steps[s]
                 made[(n, step)] = multiply_tap(n, TAP_ORDER[n][step], WHO[n][step], s < SBUF_W_STEPS)
+            if s == len(steps) - 1:
+                quantise_x()
+                for h in range(HALVES):
+                    quantise_gxi(h, state["earlier"][1], state["earlier"][2], state["earlier"][3])
             if s >= LAG:
                 consume(steps[s - LAG][0], steps[s - LAG][1])
         gxi_t, gxi_grouped, gxi_codes, gxi_scales = state["pass"]
         for h in range(HALVES):
             back_to_pixels(h, gxi_t, gxi_grouped, True)
+        multiply_pass(0, state["earlier"][2], state["earlier"][3])
         for h in range(HALVES):
             quantise_gxi(h, gxi_grouped, gxi_codes, gxi_scales)
         multiply_pass(PASSES - 1, gxi_codes, gxi_scales)

@@ -41,9 +41,10 @@ FLOPS = 2 * IMAGES * IMAGE_PIXELS * X_CH * CH + 2 * IMAGES * IMAGE_PIXELS * CH *
 BYTES = 2 * IMAGES * IMAGE_PIXELS * (X_CH + CH + GROUPS * TAPS) + 4 * X_CH * CH
 
 MIDDLE = 4
-TAP_ORDER = ((4, 3, 0, 5, 2, 1, 8, 6, 7), (4, 1, 3, 0, 5, 2, 6, 8, 7))
-WHO = (("V", "V", "S", "V", "V", "G", "S", "V", "V"), ("V", "G", "V", "S", "V", "G", "V", "VG", "V"))
+TAP_ORDER = ((4, 3, 0, 5, 2, 6, 1, 8, 7), (4, 1, 3, 0, 5, 2, 6, 8, 7))
+WHO = (("V", "V", "S", "V", "V", "V", "G", "VS", "V"), ("V", "G", "V", "S", "V", "G", "V", "VG", "V"))
 LAG = 3
+GATE = 1
 KICKS = (4, 2)
 SBUF_W_STEPS = 2
 
@@ -83,10 +84,11 @@ def tile_involution2d_pa_s_kernel(tc, x, Wi, bi, w_span, grad_out, out):
         ctx.enter_context(tc.manual_schedule(engines={mybir.EngineType.PE}))
         keep = ctx.enter_context(tc.tile_pool(name="keep", bufs=1))
         products = {
-            "V": ctx.enter_context(tc.tile_pool(name="v_products", bufs=6)),
+            "V": ctx.enter_context(tc.tile_pool(name="v_products", bufs=7)),
             "G": ctx.enter_context(tc.tile_pool(name="g_products", bufs=3)),
             "S": ctx.enter_context(tc.tile_pool(name="s_products", bufs=3)),
             "VG": ctx.enter_context(tc.tile_pool(name="vg_products", bufs=1)),
+            "VS": ctx.enter_context(tc.tile_pool(name="vs_products", bufs=1)),
         }
         per_pass = ctx.enter_context(tc.tile_pool(name="per_pass", bufs=2))
         sums_psum = ctx.enter_context(tc.psum_pool(name="sums_psum", bufs=6))
@@ -173,9 +175,9 @@ def tile_involution2d_pa_s_kernel(tc, x, Wi, bi, w_span, grad_out, out):
         w_sb_halves = w_sb[:].rearrange("p (b h) f -> p b h f", h=IMAGE_TILES)
         masked = {}
 
-        def make_masks(n):
+        def make_masks(n, engines):
             images = slice(n * PASS_IMAGES, (n + 1) * PASS_IMAGES)
-            for t, who in [(t, who) for t, whos in zip(TAP_ORDER[n], WHO[n]) for who in sorted(set(whos))]:
+            for t, who in [(t, who) for t, whos in zip(TAP_ORDER[n], WHO[n]) for who in sorted(set(whos)) if who in engines]:
                 if who == "V":
                     if t == MIDDLE:
                         continue
@@ -272,7 +274,7 @@ def tile_involution2d_pa_s_kernel(tc, x, Wi, bi, w_span, grad_out, out):
         def round_sums(h, sums, gxi_t, last):
             for image_in_pass in range(PASS_IMAGES):
                 word_rows = slice(image_in_pass * IMAGE_WORD_ROWS, (image_in_pass + 1) * IMAGE_WORD_ROWS)
-                copy_out = nc.vector.tensor_copy if (last and image_in_pass == 1) else nc.scalar.copy
+                copy_out = nc.vector.tensor_copy if ((last or False) and image_in_pass == 1) else nc.scalar.copy
                 copy_out(
                     out=gxi_t[:, h * BANK_CH_TILES : (h + 1) * BANK_CH_TILES, :, word_rows],
                     in_=sums[image_in_pass][h][:].rearrange("c t (a j) -> c t j a", j=PACK),
@@ -328,6 +330,8 @@ def tile_involution2d_pa_s_kernel(tc, x, Wi, bi, w_span, grad_out, out):
         state = {}
 
         def kick(times, prod):
+            if times == 0:
+                return
             kick_bank = back_psum.tile([P, P], F32, name="back")
             for k in range(times):
                 nc.tensor.matmul(
@@ -350,7 +354,7 @@ def tile_involution2d_pa_s_kernel(tc, x, Wi, bi, w_span, grad_out, out):
                     for k in range(HALVES * PASS_IMAGES)
                 ]
                 state["sums"] = [[by_bank[h * PASS_IMAGES + image] for h in range(HALVES)] for image in range(PASS_IMAGES)]
-                kick(KICKS[n], made[steps[LAG]] if n == 0 else prod)
+                kick(KICKS[n], made[steps[GATE]] if n == 0 else made[(n - 1, TAPS - 1)])
             gxi_t, gxi_grouped, gxi_codes, gxi_scales = state["pass"]
             sums = state["sums"]
             for h in range(HALVES):
@@ -366,15 +370,21 @@ def tile_involution2d_pa_s_kernel(tc, x, Wi, bi, w_span, grad_out, out):
                 state["earlier"] = state["pass"]
 
 
-        make_masks(0)
+        make_masks(0, "VGS")
         for s in range(len(steps) + LAG):
+            if s == 8:
+                make_masks(1, "S")
+                for step in range(TAPS):
+                    if WHO[1][step] == "S":
+                        made[(1, step)] = multiply_tap(1, TAP_ORDER[1][step], "S", False)
             if s == 6:
-                make_masks(1)
-            if s == 9:
+                make_masks(1, "VG")
+            if s == 14:
                 group_x()
             if s < len(steps):
                 n, step = steps[s]
-                made[(n, step)] = multiply_tap(n, TAP_ORDER[n][step], WHO[n][step], s < SBUF_W_STEPS)
+                if (n, step) not in made:
+                    made[(n, step)] = multiply_tap(n, TAP_ORDER[n][step], WHO[n][step], s < SBUF_W_STEPS)
             if s == len(steps) - 1:
                 quantise_x()
                 for h in range(HALVES):

from contextlib import ExitStack

import concourse.mybir as mybir
from concourse.masks import make_identity

F32 = mybir.dt.float32
BF16 = mybir.dt.bfloat16
U32 = mybir.dt.uint32
U8 = mybir.dt.uint8
E4M3_X4 = mybir.dt.float8_e4m3fn_x4
E5M2_X4 = mybir.dt.float8_e5m2_x4
COPY = mybir.ActivationFunctionType.Copy

P = 128
IMAGES, ROWS, COLS = 4, 8, 32
X_CH = 256
CH = 512
GROUPS = 16
GROUP_CH = CH // GROUPS
KERNEL = 3
TAPS = KERNEL * KERNEL
TILE_ROWS = P // COLS
IMAGE_TILES = ROWS // TILE_ROWS
IMAGE_PIXELS = ROWS * COLS
TILES = IMAGES * IMAGE_TILES
BANK_CH_TILES = 2
HALF_CH = BANK_CH_TILES * P
HALVES = CH // HALF_CH
PACK = 4
PASSES = IMAGES * IMAGE_PIXELS // (P * PACK)
PASS_IMAGES = IMAGES // PASSES
PASS_TILES = PASS_IMAGES * IMAGE_TILES
IMAGE_WORD_ROWS = IMAGE_PIXELS // PACK

TAP_CH = CH // TAPS + 2
ROW = CH // TAPS + 1
PLACES = TAPS * ROW
PROD_W = 528

FLOPS = 2 * IMAGES * IMAGE_PIXELS * X_CH * CH + 2 * IMAGES * IMAGE_PIXELS * CH * TAPS
BYTES = 2 * IMAGES * IMAGE_PIXELS * (X_CH + CH + GROUPS * TAPS) + 4 * X_CH * CH

MIDDLE = 4
TAP_ORDER = ((4, 3, 0, 5, 2, 6, 1, 8, 7), (4, 1, 3, 0, 5, 2, 6, 8, 7))
WHO = (("V", "V", "S", "V", "V", "V", "G", "VS", "V"), ("V", "G", "V", "S", "V", "G", "V", "VG", "V"))
LAG = 3
GATE = 1
KICKS = (4, 2)
SBUF_W_STEPS = 2

PSUM_W = 128
PSUM_W_FIRST = GROUPS * TAPS - PSUM_W
PSUM_W_BLOCKS = TILES * PSUM_W // P


def tap_channels(t):
    first = (TAP_CH - 1) * t - 1
    return first, max(first, 0), min(first + TAP_CH, CH)


def tap_groups(t):
    first, ch_lo, ch_hi = tap_channels(t)
    return ch_lo // GROUP_CH, (ch_hi - 1) // GROUP_CH + 1


def tap_pieces(t):
    q, m0 = divmod(t * CH, TAPS)
    runs = [(0, TAPS - m0, m0, q)]
    if m0:
        runs.append((TAPS - m0, m0, 0, q + 1))
    pieces = []
    for r0, rows, m_first, q_run in runs:
        end = min(q_run + ROW, CH)
        for group in range(q_run // GROUP_CH, (end - 1) // GROUP_CH + 1):
            lo = max(q_run, group * GROUP_CH)
            hi = min(end, (group + 1) * GROUP_CH)
            pieces.append((r0, rows, m_first, group, lo - q_run, lo, hi))
    return pieces


def tile_involution2d_pa_s_kernel(tc, x, Wi, bi, w_span, grad_out, out):
    nc = tc.nc
    with ExitStack() as ctx:
        ctx.enter_context(tc.manual_schedule(engines={mybir.EngineType.PE}))
        keep = ctx.enter_context(tc.tile_pool(name="keep", bufs=1))
        products = {
            "V": ctx.enter_context(tc.tile_pool(name="v_products", bufs=7)),
            "G": ctx.enter_context(tc.tile_pool(name="g_products", bufs=3)),
            "S": ctx.enter_context(tc.tile_pool(name="s_products", bufs=3)),
            "VG": ctx.enter_context(tc.tile_pool(name="vg_products", bufs=1)),
            "VS": ctx.enter_context(tc.tile_pool(name="vs_products", bufs=1)),
        }
        per_pass = ctx.enter_context(tc.tile_pool(name="per_pass", bufs=2))
        sums_psum = ctx.enter_context(tc.psum_pool(name="sums_psum", bufs=6))
        back_psum = ctx.enter_context(tc.psum_pool(name="back_psum", bufs=1))
        w_psum = ctx.enter_context(tc.psum_pool(name="w_psum", bufs=1))

        g_rows = grad_out.rearrange("b h w f -> (b h w) f").rearrange("(u p) f -> p u f", p=P)
        w_rows = w_span.rearrange("b h w f -> (b h w) f").rearrange("(u p) f -> p u f", p=P)
        g_sb = keep.tile([P, TILES, CH], BF16)
        w_sb = keep.tile([P, TILES, GROUPS * TAPS], BF16)
        w_c = keep.tile([P, TILES, PSUM_W], BF16)
        x_raw = keep.tile([P, PASSES, PACK, X_CH], BF16)

        def load_g(image):
            tiles = slice(image * IMAGE_TILES, (image + 1) * IMAGE_TILES)
            nc.sync.dma_start(out=g_sb[:, tiles, :], in_=g_rows[:, tiles, :])

        nc.sync.dma_start(out=w_sb[:], in_=w_rows)
        load_g(0)
        load_g(1)
        nc.sync.dma_start(out=w_c[:], in_=w_rows[:, :, PSUM_W_FIRST:])
        load_g(2)
        load_g(3)
        nc.sync.dma_start(
            out=x_raw[:],
            in_=x.rearrange("b h w k -> (b h w) k").rearrange("(n p j) k -> p n j k", p=P, j=PACK),
        )

        warm = keep.tile([P, 2], F32)
        nc.vector.memset(warm[:], 0.0)
        nc.scalar.activation(out=warm[:, 1:2], in_=warm[:, 0:1], func=COPY)

        ident_twice = keep.tile([P, 2 * P], F32)
        make_identity(nc, ident_twice[:, 0:P])
        ident_bf16 = keep.tile([P, P], BF16)
        nc.vector.tensor_copy(out=ident_bf16[:], in_=ident_twice[:, 0:P])
        nc.vector.tensor_copy(out=ident_twice[:, P : 2 * P], in_=ident_twice[:, 0:P])

        ident_by_col = ident_twice[:, 0:P].rearrange("k (r s) -> k s r", s=COLS)
        on_edge = keep.tile([P, 2], F32)
        nc.vector.tensor_reduce(
            out=on_edge[:, 0:1], in_=ident_by_col[:, 0, :], axis=mybir.AxisListType.X, op=mybir.AluOpType.add
        )
        nc.vector.tensor_reduce(
            out=on_edge[:, 1:2],
            in_=ident_by_col[:, COLS - 1, :],
            axis=mybir.AxisListType.X,
            op=mybir.AluOpType.add,
        )
        off_edge = keep.tile([P, 2], F32)
        nc.vector.tensor_scalar(
            out=off_edge[:],
            in0=on_edge[:],
            scalar1=-1.0,
            scalar2=1.0,
            op0=mybir.AluOpType.mult,
            op1=mybir.AluOpType.add,
        )
        has_neighbour = keep.tile([P, IMAGE_TILES, KERNEL, KERNEL], F32)
        nc.vector.memset(has_neighbour[:], 1.0)
        for j, edge in ((0, 0), (KERNEL - 1, 1)):
            nc.vector.tensor_copy(
                out=has_neighbour[:, :, :, j],
                in_=off_edge[:, edge : edge + 1].unsqueeze(2).to_broadcast([P, IMAGE_TILES, KERNEL]),
            )
        nc.vector.memset(has_neighbour[0:COLS, 0, 0, :], 0.0)
        nc.vector.memset(has_neighbour[P - COLS : P, IMAGE_TILES - 1, KERNEL - 1, :], 0.0)

        def mask_of(t, half):
            return has_neighbour[:, half, t // KERNEL, t % KERNEL : t % KERNEL + 1]

        w_c_flat = w_c[:].rearrange("p u f -> p (u f)")
        w_t_ps = back_psum.tile([P, PSUM_W_BLOCKS, P], BF16, name="back")
        for k in range(PSUM_W_BLOCKS):
            nc.tensor.transpose(w_t_ps[:, k, :], w_c_flat[:, k * P : (k + 1) * P], ident_bf16[:])
        w_t = keep.tile([P, PSUM_W_BLOCKS, P], BF16)
        nc.scalar.copy(out=w_t[:], in_=w_t_ps[:])
        w_ps = w_psum.tile([P, TILES, PSUM_W], BF16, name="w_bank")
        w_ps_flat = w_ps[:].rearrange("p u f -> p (u f)")
        for k in range(PSUM_W_BLOCKS):
            nc.tensor.transpose(w_ps_flat[:, k * P : (k + 1) * P], w_t[:, k, :], ident_bf16[:])

        g_sb_halves = g_sb[:].rearrange("p (b h) f -> p b h f", h=IMAGE_TILES)
        w_sb_halves = w_sb[:].rearrange("p (b h) f -> p b h f", h=IMAGE_TILES)
        masked = {}

        def make_masks(n, engines):
            images = slice(n * PASS_IMAGES, (n + 1) * PASS_IMAGES)
            for t, who in [(t, who) for t, whos in zip(TAP_ORDER[n], WHO[n]) for who in sorted(set(whos)) if who in engines]:
                if who == "V":
                    if t == MIDDLE:
                        continue
                    first, ch_lo, ch_hi = tap_channels(t)
                    masked[(t, n, who)] = keep.tile([P, PASS_TILES, TAP_CH], BF16, name="g_tap%d_%d" % (t, n))
                    src, cols_in, cols_out = g_sb_halves, slice(ch_lo, ch_hi), slice(ch_lo - first, ch_hi - first)
                else:
                    dtype = BF16 if who == "G" else F32
                    masked[(t, n, who)] = keep.tile([P, PASS_TILES, GROUPS * TAPS], dtype, name="w_tap%d_%d" % (t, n))
                    cols_in = slice(tap_groups(t)[0] * TAPS, tap_groups(t)[1] * TAPS)
                    src, cols_out = w_sb_halves, cols_in
                by_half = masked[(t, n, who)][:].rearrange("p (b h) f -> p b h f", h=IMAGE_TILES)
                for half in range(IMAGE_TILES):
                    nc.scalar.activation(
                        out=by_half[:, :, half, cols_out],
                        in_=src[:, images, half, cols_in],
                        func=COPY,
                        scale=mask_of(t, half),
                    )

        x_grouped = keep.tile([P, PASSES, X_CH, PACK], BF16, align_bytes=64)
        x_codes = keep.tile([P, PASSES, X_CH], U32, align_bytes=64)
        x_scales = keep.tile([P, PASSES, X_CH], U8, align_bytes=64)

        def group_x():
            for n in range(PASSES):
                nc.scalar.copy(out=x_grouped[:, n], in_=x_raw[:, n].rearrange("p j k -> p k j"))

        def quantise_x():
            nc.vector.quantize_mx(
                out=x_codes[:].rearrange("p n k -> p (n k)").bitcast(E4M3_X4),
                scales=x_scales[:].rearrange("p n k -> p (n k)"),
                in_=x_grouped[:].rearrange("p n k j -> p (n k j)"),
            )

        def multiply_tap(n, t, whos, w_from_sbuf):
            prod = products[whos].tile([P, PASS_TILES, PROD_W], F32, name="prod_" + whos)
            by_row = prod[:, :, 0:PLACES].rearrange("p u (r i) -> p u r i", i=ROW)
            first = tap_channels(t)[0]
            share = PASS_TILES // len(whos)
            for k_who, who in enumerate(whos):
                mine = slice(k_who * share, (k_who + 1) * share)
                tiles = slice(n * PASS_TILES + mine.start, n * PASS_TILES + mine.stop)
                for r0, rows, m_first, group, i0, lo, hi in tap_pieces(t):
                    weights = slice(group * TAPS + m_first, group * TAPS + m_first + rows)
                    if who == "S":
                        for u in range(mine.start, mine.stop):
                            for k in range(rows):
                                nc.scalar.activation(
                                    out=by_row[:, u, r0 + k, i0 : i0 + hi - lo],
                                    in_=g_sb[:, n * PASS_TILES + u, lo:hi],
                                    func=COPY,
                                    scale=masked[(t, n, who)][:, u, weights.start + k : weights.start + k + 1],
                                )
                        continue
                    shape = [P, share, rows, hi - lo]
                    if who == "G":
                        engine, g_part, w_part = nc.gpsimd, g_sb[:, tiles, lo:hi], masked[(t, n, who)][:, mine, weights]
                    else:
                        engine = nc.vector
                        if t == MIDDLE:
                            g_part = g_sb[:, tiles, lo:hi]
                        else:
                            g_part = masked[(t, n, who)][:, mine, lo - first : hi - first]
                        if w_from_sbuf:
                            w_part = w_sb[:, tiles, weights]
                        else:
                            w_part = w_ps[:, tiles, weights.start - PSUM_W_FIRST : weights.stop - PSUM_W_FIRST]
                    engine.tensor_tensor(
                        out=by_row[:, mine, r0 : r0 + rows, i0 : i0 + hi - lo],
                        in0=g_part.unsqueeze(2).to_broadcast(shape),
                        in1=w_part.unsqueeze(3).to_broadcast(shape),
                        op=mybir.AluOpType.mult,
                    )
            return prod

        def add_tap(bank, h, prod, image_in_pass, t, first_tap, last_tap):
            i, j = t // KERNEL, t % KERNEL
            for ct in range(BANK_CH_TILES):
                for half in range(IMAGE_TILES):
                    wanted = half * P + (i - 1) * COLS
                    start_pixel = min(max(wanted, 0), IMAGE_PIXELS - P)
                    turn = (start_pixel - wanted - (j - 1)) % P
                    place = (h * BANK_CH_TILES + ct) * P
                    nc.tensor.matmul(
                        out=bank[:, ct, start_pixel : start_pixel + P],
                        lhsT=prod[:, image_in_pass * IMAGE_TILES + half, place : place + P],
                        rhs=ident_twice[:, turn : turn + P],
                        is_transpose=True,
                        start=(first_tap and half == 0 and ct == 0),
                        stop=(last_tap and half == IMAGE_TILES - 1 and ct == BANK_CH_TILES - 1),
                    )

        def round_sums(h, sums, gxi_t, last):
            for image_in_pass in range(PASS_IMAGES):
                word_rows = slice(image_in_pass * IMAGE_WORD_ROWS, (image_in_pass + 1) * IMAGE_WORD_ROWS)
                copy_out = nc.vector.tensor_copy if ((last or False) and image_in_pass == 1) else nc.scalar.copy
                copy_out(
                    out=gxi_t[:, h * BANK_CH_TILES : (h + 1) * BANK_CH_TILES, :, word_rows],
                    in_=sums[image_in_pass][h][:].rearrange("c t (a j) -> c t j a", j=PACK),
                )

        def back_to_pixels(h, gxi_t, gxi_grouped, last):
            if last and h == 1:
                back = w_psum.tile([P, PACK, HALF_CH], BF16, name="w_bank")
            else:
                back = back_psum.tile([P, PACK, HALF_CH], BF16, name="back")
            for ct in range(BANK_CH_TILES):
                for j in range(PACK):
                    nc.tensor.transpose(
                        back[:, j, ct * P : (ct + 1) * P], gxi_t[:, h * BANK_CH_TILES + ct, j, :], ident_bf16[:]
                    )
            copy_out = nc.vector.tensor_copy if (last and h == 1) else nc.scalar.copy
            copy_out(
                out=gxi_grouped[:, h * HALF_CH : (h + 1) * HALF_CH, :],
                in_=back[:].rearrange("p j c -> p c j"),
            )

        def quantise_gxi(h, gxi_grouped, gxi_codes, gxi_scales):
            half_ch = slice(h * HALF_CH, (h + 1) * HALF_CH)
            nc.vector.quantize_mx(
                out=gxi_codes[:, half_ch].bitcast(E5M2_X4),
                scales=gxi_scales[:, half_ch],
                in_=gxi_grouped[:, half_ch, :].rearrange("p c j -> p (c j)"),
            )

        out_acc = []

        def multiply_pass(n, gxi_codes, gxi_scales):
            if n == 0:
                out_acc.extend(sums_psum.tile([P, CH], F32, name="sums") for m in range(X_CH // P))
            for m in range(X_CH // P):
                nc.tensor.matmul_mx(
                    out=out_acc[m][:],
                    lhsT=x_codes[:, n, m * P : (m + 1) * P].bitcast(E4M3_X4),
                    lhsT_scale=x_scales[:, n, m * P : (m + 1) * P],
                    rhs=gxi_codes[:].bitcast(E5M2_X4),
                    rhs_scale=gxi_scales[:],
                    start=(n == 0),
                    stop=(n == PASSES - 1),
                )

        later = {}

        def at(n, step, call):
            later.setdefault((n, step), []).append(call)

        steps = [(n, step) for n in range(PASSES) for step in range(TAPS)]
        made = {}
        state = {}

        def kick(times, prod):
            if times == 0:
                return
            kick_bank = back_psum.tile([P, P], F32, name="back")
            for k in range(times):
                nc.tensor.matmul(
                    out=kick_bank[:], lhsT=ident_twice[:, 0:P], rhs=prod[:, 0, 0:P], start=True, stop=True
                )

        def consume(n, step):
            t = TAP_ORDER[n][step]
            prod = made[(n, step)]
            last = n == PASSES - 1
            if step == 0:
                state["pass"] = (
                    per_pass.tile([P, CH // P, PACK, P], BF16, name="gxi_t"),
                    per_pass.tile([P, CH, PACK], BF16, name="gxi_grouped", align_bytes=64),
                    per_pass.tile([P, CH], U32, name="gxi_codes", align_bytes=64),
                    per_pass.tile([P, CH], U8, name="gxi_scales", align_bytes=64),
                )
                by_bank = [
                    sums_psum.tile([P, BANK_CH_TILES, IMAGE_PIXELS], F32, name="sums")
                    for k in range(HALVES * PASS_IMAGES)
                ]
                state["sums"] = [[by_bank[h * PASS_IMAGES + image] for h in range(HALVES)] for image in range(PASS_IMAGES)]
                kick(KICKS[n], made[steps[GATE]] if n == 0 else made[(n - 1, TAPS - 1)])
            gxi_t, gxi_grouped, gxi_codes, gxi_scales = state["pass"]
            sums = state["sums"]
            for h in range(HALVES):
                for image_in_pass in range(PASS_IMAGES):
                    add_tap(sums[image_in_pass][h], h, prod, image_in_pass, t, step == 0, step == TAPS - 1)
                if step == TAPS - 1:
                    round_sums(h, sums, gxi_t, last)
            for call in later.get((n, step), []):
                call()
            if step == TAPS - 1 and not last:
                at(n + 1, 0, lambda a=gxi_t, b=gxi_grouped: back_to_pixels(0, a, b, False))
                at(n + 1, 2, lambda a=gxi_t, b=gxi_grouped: back_to_pixels(1, a, b, False))
                state["earlier"] = state["pass"]


        make_masks(0, "VGS")
        for s in range(len(steps) + LAG):
            if s == 8:
                make_masks(1, "S")
                for step in range(TAPS):
                    if WHO[1][step] == "S":
                        made[(1, step)] = multiply_tap(1, TAP_ORDER[1][step], "S", False)
            if s == 6:
                make_masks(1, "VG")
            if s == 14:
                group_x()
            if s < len(steps):
                n, step = steps[s]
                if (n, step) not in made:
                    made[(n, step)] = multiply_tap(n, TAP_ORDER[n][step], WHO[n][step], s < SBUF_W_STEPS)
            if s == len(steps) - 1:
                quantise_x()
                for h in range(HALVES):
                    quantise_gxi(h, state["earlier"][1], state["earlier"][2], state["earlier"][3])
            if s >= LAG:
                consume(steps[s - LAG][0], steps[s - LAG][1])
        gxi_t, gxi_grouped, gxi_codes, gxi_scales = state["pass"]
        for h in range(HALVES):
            back_to_pixels(h, gxi_t, gxi_grouped, True)
        multiply_pass(0, state["earlier"][2], state["earlier"][3])
        for h in range(HALVES):
            quantise_gxi(h, gxi_grouped, gxi_codes, gxi_scales)
        multiply_pass(PASSES - 1, gxi_codes, gxi_scales)

        for m in range(X_CH // P):
            result = keep.tile([P, PLACES], F32, name="result%d" % m)
            by_channel = result[:].rearrange("p (i r) -> p i r", r=TAPS)
            copy_out = nc.scalar.copy if m % 2 == 0 else nc.vector.tensor_copy
            queue = nc.scalar if m % 2 == 0 else nc.sync
            copy_out(
                out=by_channel[:, :, 0 : TAPS - 1],
                in_=out_acc[m][:, 0 : (TAPS - 1) * ROW].rearrange("p (r i) -> p i r", i=ROW),
            )
            copy_out(out=by_channel[:, 0 : ROW - 1, TAPS - 1], in_=out_acc[m][:, (TAPS - 1) * ROW : CH])
            queue.dma_start(out=out[m * P : (m + 1) * P, :], in_=result[:, 0:CH])
